import numpy as np
import ml_dtypes


def mxq(x, axis, fmt="e4m3"):
    dtype, down = {"e4m3": (ml_dtypes.float8_e4m3fn, 7), "e5m2": (ml_dtypes.float8_e5m2, 14)}[fmt]
    v = np.moveaxis(np.asarray(x, np.float32).astype(ml_dtypes.bfloat16).astype(np.float64), axis, -1)
    blocks = v.reshape(v.shape[:-1] + (-1, 32))
    amax = np.abs(blocks).max(-1, keepdims=True)
    byte = np.maximum(np.where(amax > 0, np.frexp(amax)[1] - 1 + 127, 0) - down, 1)
    scale = np.exp2(byte - 127.0)
    codes = (blocks / scale).astype(np.float32).astype(dtype).astype(np.float64)
    return np.moveaxis((codes * scale).reshape(v.shape), -1, axis)


WIDE = False


def mx_kscale(k):
    if not WIDE:
        return np.ones(k)
    levels = np.array([10, -10, 5, -5, 0])
    a = np.random.permutation(np.resize(levels, k // 512 * 4)).reshape(k // 512, 4)
    idx = np.arange(k)
    return np.exp2(a[idx // 512, idx % 128 // 32])


BF16 = ml_dtypes.bfloat16


def bf(x):
    return np.asarray(x, np.float32).astype(BF16)


def f64(x):
    return np.asarray(x).astype(np.float64)


E2M1 = np.array([0.0, 0.5, 1.0, 1.5, 2.0, 3.0, 4.0, 6.0, -0.0, -0.5, -1.0, -1.5, -2.0, -3.0, -4.0, -6.0])


def pack_weight(w, fmt):
    k, n = w.shape
    w = f64(bf(w)).reshape(k // 32, 32, n)
    amax = np.abs(w).max(1)
    if fmt == "e4m3":
        byte = np.frexp(amax)[1] - 1 + 127 - 7
    else:
        mant, ex = np.frexp(amax / 6.0)
        byte = np.where(mant > 0.5, ex, ex - 1) + 127
    byte = np.clip(np.where(amax > 0, byte, 1), 1, 254)
    scaled = (w * np.exp2(127.0 - byte)[:, None, :]).reshape(k, n).astype(np.float32)
    by_word = np.ascontiguousarray(scaled.reshape(k // 512, 128, 4, n).transpose(0, 1, 3, 2))
    if fmt == "e4m3":
        words = by_word.astype(ml_dtypes.float8_e4m3fn).view(np.uint8)
    else:
        c = by_word.astype(ml_dtypes.float4_e2m1fn).view(np.uint8) & 0xF
        words = c[..., 0::2] | (c[..., 1::2] << 4)
    return np.ascontiguousarray(words), np.ascontiguousarray(byte.astype(np.uint8).reshape(k // 512, 16, n))


def unpack_weight(words, scales, fmt):
    g, p, n, _ = words.shape
    if fmt == "e4m3":
        vals = np.ascontiguousarray(words).view(ml_dtypes.float8_e4m3fn).astype(np.float64)
    else:
        nib = np.empty((g, p, n, 4), np.uint8)
        nib[..., 0::2] = words & 0xF
        nib[..., 1::2] = words >> 4
        vals = E2M1[nib]
    vals = vals * np.repeat(np.exp2(scales.astype(np.float64) - 127.0), 8, axis=1)[..., None]
    return vals.transpose(0, 1, 3, 2).reshape(g * 512, n)


B, I, H, P = 512, 1024, 1024, 2048


def sigmoid(v):
    return 1.0 / (1.0 + np.exp(-v))


def setup_inputs():
    s = mx_kscale(H)
    s = s * np.exp2(-np.round(np.log2(s.mean())))
    hidden_new = bf((1.6 + 1.5 * np.random.standard_normal((B, H))) * s)
    persistent_memory = bf(0.2 * np.random.standard_normal((B, P)))
    Waddr_words, Waddr_scales = pack_weight((np.random.standard_normal((P, H)) * 3.0 / np.sqrt(H) / s[None, :]).T, "e4m3")
    baddr = bf(np.random.standard_normal(P))
    Wwrite_words, Wwrite_scales = pack_weight((np.random.standard_normal((P, H)) * 0.7 / np.sqrt(H) / s[None, :]).T, "e4m3")
    bwrite = bf(np.random.standard_normal(P))
    Wforget_words, Wforget_scales = pack_weight((np.random.standard_normal((P, H)) * 0.7 / np.sqrt(H) / s[None, :]).T, "e4m3")
    bforget = bf(1.0 + 0.3 * np.random.standard_normal(P))
    return {"hidden_new": hidden_new,
            "persistent_memory": persistent_memory,
            "Waddr_words": Waddr_words,
            "Waddr_scales": Waddr_scales,
            "baddr": baddr,
            "Wwrite_words": Wwrite_words,
            "Wwrite_scales": Wwrite_scales,
            "bwrite": bwrite,
            "Wforget_words": Wforget_words,
            "Wforget_scales": Wforget_scales,
            "bforget": bforget}


def reference(hidden_new, persistent_memory, Waddr_words, Waddr_scales, baddr, Wwrite_words, Wwrite_scales, bwrite, Wforget_words, Wforget_scales, bforget):
    hn = f64(hidden_new)
    hq = mxq(hn, 1, "e4m3")
    z = (hq @ unpack_weight(Waddr_words, Waddr_scales, "e4m3")) + f64(baddr)
    e = np.exp(z - z.max(axis=1, keepdims=True))
    addr = e / e.sum(axis=1, keepdims=True)
    write = sigmoid((hq @ unpack_weight(Wwrite_words, Wwrite_scales, "e4m3")) + f64(bwrite))
    forget = sigmoid((hq @ unpack_weight(Wforget_words, Wforget_scales, "e4m3")) + f64(bforget))
    hp = np.mean(hn, axis=1, keepdims=True)
    return forget * f64(persistent_memory) + write * hp * addr

@@ -1,0 +1,282 @@
+from contextlib import ExitStack
+
+import concourse.mybir as mybir
+from concourse.masks import make_identity
+
+F32 = mybir.dt.float32
+BF16 = mybir.dt.bfloat16
+I32 = mybir.dt.int32
+U32 = mybir.dt.uint32
+U8 = mybir.dt.uint8
+FP8X4 = mybir.dt.float8_e4m3fn_x4
+ALU = mybir.AluOpType
+ACT = mybir.ActivationFunctionType
+
+P = 128
+BATCH = 512
+HIDDEN = 1024
+SLOTS = 2048
+ROW_TILES = BATCH // P
+PACK = 4
+K_PASS = P * PACK
+PASSES = HIDDEN // K_PASS
+BANK = 512
+CHUNKS = SLOTS // BANK
+BLOCKS = BANK // P
+PLANE_ROWS = 4
+QUADRANTS = 4
+
+FLOPS = 3 * 2 * BATCH * HIDDEN * SLOTS
+
+
+def chunk_cols(c):
+    return slice(c * BANK, (c + 1) * BANK)
+
+
+def block_cols(i):
+    return slice(i * P, (i + 1) * P)
+
+
+def tile_persistentgrucell_pc_kernel(
+    tc,
+    hidden_new,
+    persistent_memory,
+    Waddr_words,
+    Waddr_scales,
+    baddr,
+    Wwrite_words,
+    Wwrite_scales,
+    bwrite,
+    Wforget_words,
+    Wforget_scales,
+    bforget,
+    out,
+):
+    nc = tc.nc
+    hidden_rows = hidden_new.rearrange("(p t) k -> p t k", t=ROW_TILES)
+    memory_rows = persistent_memory.rearrange("(p t) n -> p t n", t=ROW_TILES)
+    out_rows = out.rearrange("(p t) n -> p t n", t=ROW_TILES)
+
+    with ExitStack() as stack:
+        keep = stack.enter_context(tc.tile_pool(name="keep", bufs=1))
+        gate_pool = stack.enter_context(tc.tile_pool(name="gate", bufs=3))
+        term_pool = stack.enter_context(tc.tile_pool(name="term", bufs=4))
+        acc_pool = stack.enter_context(tc.psum_pool(name="acc", bufs=4))
+        turn_pool = stack.enter_context(tc.psum_pool(name="turn", bufs=4))
+
+        hidden_sb = keep.tile([P, ROW_TILES, HIDDEN], BF16)
+        grouped = keep.tile([P, PASSES, BATCH, PACK], BF16, align_bytes=64)
+        h_codes = keep.tile([P, PASSES, BATCH], U32, align_bytes=64)
+        h_scales = keep.tile([P, PASSES, BATCH], U8, align_bytes=64)
+        wa_words = keep.tile([P, PASSES, SLOTS], U32, align_bytes=64)
+        wf_words = keep.tile([P, PASSES, SLOTS], U32, align_bytes=64)
+        ww_words = keep.tile([P, PASSES, SLOTS], U32, align_bytes=64)
+        planes_af = keep.tile([P, SLOTS], U8, align_bytes=64)
+        planes_w = keep.tile([P, SLOTS], U8, align_bytes=64)
+        memory_sb = keep.tile([P, ROW_TILES, SLOTS], BF16)
+        addr = keep.tile([P, ROW_TILES, SLOTS], F32)
+        result = keep.tile([P, ROW_TILES, SLOTS], F32)
+        identity = keep.tile([P, P], F32)
+        ones = keep.tile([P, P], BF16)
+        baddr_row = keep.tile([P, SLOTS], BF16)
+        baddr_all = keep.tile([P, SLOTS], F32)
+        gate_bias_rows = keep.tile([P, P], BF16)
+        gate_bias_rows_f32 = keep.tile([P, P], F32)
+        half_gate_bias = keep.tile([P, 2 * CHUNKS * BLOCKS], F32)
+        scaled_hidden = keep.tile([P, ROW_TILES, HIDDEN], BF16)
+        half_mean = keep.tile([P, ROW_TILES], F32)
+        neg_max = keep.tile([P, ROW_TILES], F32)
+        exp_sum = keep.tile([P, ROW_TILES], F32)
+        inv_sum = keep.tile([P, ROW_TILES], F32)
+
+        nc.vector.memset(planes_af[:].bitcast(I32), 0)
+        nc.vector.memset(planes_w[:].bitcast(I32), 0)
+        nc.vector.memset(gate_bias_rows[:], 0.0)
+        nc.vector.memset(baddr_row[:], 0.0)
+        nc.vector.memset(ones[:], 1.0)
+        make_identity(nc, identity[:])
+
+        def load_words(dst, words, c):
+            view = words.rearrange("g p n j -> g p (n j)").bitcast(I32).rearrange("g p n -> p g n")
+            nc.sync.dma_start(out=dst[:, :, chunk_cols(c)].bitcast(I32), in_=view[:, :, chunk_cols(c)])
+
+        def load_scales(planes, first_row, scales):
+            rows = scales.bitcast(I32)
+            for quadrant in range(QUADRANTS):
+                start = 32 * quadrant + first_row
+                nc.sync.dma_start(
+                    out=planes[start : start + PASSES * PLANE_ROWS, :].bitcast(I32),
+                    in_=rows[:, PLANE_ROWS * quadrant : PLANE_ROWS * (quadrant + 1), :],
+                )
+
+        for t in range(ROW_TILES):
+            nc.sync.dma_start(out=hidden_sb[:, t, :], in_=hidden_rows[:, t, :])
+        nc.scalar.dma_start(out=baddr_row[0:1, :], in_=baddr.rearrange("(o n) -> o n", o=1))
+        nc.scalar.dma_start(out=gate_bias_rows[0:16, :], in_=bforget.rearrange("(i p) -> i p", p=P))
+        nc.scalar.dma_start(out=gate_bias_rows[16:32, :], in_=bwrite.rearrange("(i p) -> i p", p=P))
+        load_scales(planes_af, 0, Waddr_scales)
+        for c in range(CHUNKS):
+            load_words(wa_words, Waddr_words, c)
+        load_scales(planes_af, 8, Wforget_scales)
+        load_scales(planes_w, 0, Wwrite_scales)
+        for c in range(CHUNKS):
+            load_words(wf_words, Wforget_words, c)
+            nc.sync.dma_start(out=memory_sb[:, :, chunk_cols(c)], in_=memory_rows[:, :, chunk_cols(c)])
+        for c in range(CHUNKS):
+            load_words(ww_words, Wwrite_words, c)
+
+        for c in range(CHUNKS):
+            spread = acc_pool.tile([P, BANK], F32, tag="acc")
+            nc.tensor.matmul(out=spread[:], lhsT=ones[:], rhs=baddr_row[:, chunk_cols(c)], start=True, stop=True)
+            nc.vector.tensor_copy(out=baddr_all[:, chunk_cols(c)], in_=spread[:])
+        nc.vector.tensor_copy(out=gate_bias_rows_f32[:], in_=gate_bias_rows[:])
+        bias_cols = turn_pool.tile([P, BANK], F32, tag="turn")
+        nc.tensor.transpose(bias_cols[:, 0:P], gate_bias_rows_f32[:], identity[:])
+        nc.vector.tensor_scalar_mul(out=half_gate_bias[:], in0=bias_cols[:, 0 : 2 * CHUNKS * BLOCKS], scalar1=0.5)
+
+        hidden_words = hidden_sb[:].bitcast(F32)
+        grouped_words = grouped[:].bitcast(F32)
+        words_per_pass = K_PASS // 2
+        for t in range(ROW_TILES):
+            turned = turn_pool.tile([P, BANK], F32, tag="turn")
+            for g in range(PASSES):
+                for u in range(2):
+                    nc.tensor.transpose(
+                        turned[:, block_cols(2 * g + u)],
+                        hidden_words[:, t, words_per_pass * g + u : words_per_pass * (g + 1) : 2],
+                        identity[:],
+                    )
+            nc.scalar.copy(
+                out=grouped_words[:, :, block_cols(t), :],
+                in_=turned[:].rearrange("p (g u r) -> p g r u", g=PASSES, u=2),
+            )
+            for g in range(PASSES):
+                nc.vector.quantize_mx(
+                    out=h_codes[:, g, block_cols(t)].bitcast(FP8X4),
+                    scales=h_scales[:, g, block_cols(t)],
+                    in_=grouped[:, g, block_cols(t), :].rearrange("p r j -> p (r j)"),
+                )
+        for t in range(ROW_TILES):
+            nc.scalar.activation(
+                out=scaled_hidden[:, t, :],
+                in_=hidden_sb[:, t, :],
+                func=ACT.Copy,
+                scale=0.5 / HIDDEN,
+                accum_out=half_mean[:, t : t + 1],
+            )
+
+        def addr_scores(t, c):
+            acc = acc_pool.tile([P, BANK], F32, tag="acc")
+            for g in range(PASSES):
+                nc.tensor.matmul_mx(
+                    out=acc[:],
+                    lhsT=h_codes[:, g, block_cols(t)].bitcast(FP8X4),
+                    lhsT_scale=h_scales[:, g, block_cols(t)],
+                    rhs=wa_words[:, g, chunk_cols(c)].bitcast(FP8X4),
+                    rhs_scale=planes_af[PLANE_ROWS * g : P, chunk_cols(c)],
+                    start=(g == 0),
+                    stop=(g == PASSES - 1),
+                )
+            nc.vector.tensor_tensor(
+                out=addr[:, t, chunk_cols(c)], in0=acc[:], in1=baddr_all[:, chunk_cols(c)], op=ALU.add
+            )
+
+        def addr_softmax(t):
+            nc.vector.tensor_reduce(
+                out=neg_max[:, t : t + 1], in_=addr[:, t, :], axis=mybir.AxisListType.X, op=ALU.max, negate=True
+            )
+            nc.scalar.activation(
+                out=addr[:, t, :],
+                in_=addr[:, t, :],
+                func=ACT.Exp,
+                bias=neg_max[:, t : t + 1],
+                scale=1.0,
+                accum_out=exp_sum[:, t : t + 1],
+            )
+            nc.vector.reciprocal(out=inv_sum[:, t : t + 1], in_=exp_sum[:, t : t + 1])
+            nc.gpsimd.tensor_scalar(
+                out=addr[:, t, :],
+                in0=addr[:, t, :],
+                scalar1=inv_sum[:, t : t + 1],
+                scalar2=half_mean[:, t : t + 1],
+                op0=ALU.mult,
+                op1=ALU.mult,
+            )
+
+        def gate_tanh(words, planes, first_row, first_bias, c):
+            gate_t = gate_pool.tile([P, BLOCKS, BATCH], F32, tag="gate_t")
+            for i in range(BLOCKS):
+                block = BLOCKS * c + i
+                acc = acc_pool.tile([P, BANK], F32, tag="acc")
+                for g in range(PASSES):
+                    nc.tensor.matmul_mx(
+                        out=acc[:],
+                        lhsT=words[:, g, block_cols(block)].bitcast(FP8X4),
+                        lhsT_scale=planes[first_row + PLANE_ROWS * g : P, block_cols(block)],
+                        rhs=h_codes[:, g, :].bitcast(FP8X4),
+                        rhs_scale=h_scales[:, g, :],
+                        start=(g == 0),
+                        stop=(g == PASSES - 1),
+                    )
+                nc.scalar.activation(
+                    out=gate_t[:, i, :],
+                    in_=acc[:],
+                    func=ACT.Tanh,
+                    bias=half_gate_bias[:, first_bias + block : first_bias + block + 1],
+                    scale=0.5,
+                )
+            return gate_t
+
+        def turn_back(gate_t, t):
+            turned = turn_pool.tile([P, BANK], F32, tag="turn")
+            for i in range(BLOCKS):
+                nc.tensor.transpose(turned[:, block_cols(i)], gate_t[:, i, block_cols(t)], identity[:])
+            return turned
+
+        def forget_term(gate_t, c):
+            for t in range(ROW_TILES):
+                turned = turn_back(gate_t, t)
+                nc.vector.scalar_tensor_tensor(
+                    out=result[:, t, chunk_cols(c)],
+                    in0=turned[:],
+                    scalar=1.0,
+                    in1=memory_sb[:, t, chunk_cols(c)],
+                    op0=ALU.add,
+                    op1=ALU.mult,
+                )
+
+        def write_term_and_store(gate_t, c):
+            for t in range(ROW_TILES):
+                turned = turn_back(gate_t, t)
+                term = term_pool.tile([P, BANK], F32, tag="term")
+                nc.vector.scalar_tensor_tensor(
+                    out=term[:],
+                    in0=turned[:],
+                    scalar=1.0,
+                    in1=addr[:, t, chunk_cols(c)],
+                    op0=ALU.add,
+                    op1=ALU.mult,
+                )
+                nc.gpsimd.tensor_tensor(
+                    out=result[:, t, chunk_cols(c)], in0=term[:], in1=result[:, t, chunk_cols(c)], op=ALU.add
+                )
+                nc.sync.dma_start(out=out_rows[:, t, chunk_cols(c)], in_=result[:, t, chunk_cols(c)])
+
+        for pair in range(ROW_TILES // 2):
+            for c in range(CHUNKS):
+                for t in (2 * pair, 2 * pair + 1):
+                    addr_scores(t, c)
+            for t in (2 * pair, 2 * pair + 1):
+                addr_softmax(t)
+            for c in (2 * pair, 2 * pair + 1):
+                nc.gpsimd.tensor_scalar(
+                    out=memory_sb[:, :, chunk_cols(c)],
+                    in0=memory_sb[:, :, chunk_cols(c)],
+                    scalar1=0.5,
+                    scalar2=0.0,
+                    op0=ALU.mult,
+                    op1=ALU.add,
+                )
+                forget_term(gate_tanh(wf_words, planes_af, 8, 0, c), c)
+        for c in range(CHUNKS):
+            write_term_and_store(gate_tanh(ww_words, planes_w, 0, CHUNKS * BLOCKS, c), c)

@@ -21,10 +21,14 @@ PACK = 4
 K_PASS = P * PACK
 PASSES = HIDDEN // K_PASS
 BANK = 512
+PSUM_BANKS = 8
 CHUNKS = SLOTS // BANK
 BLOCKS = BANK // P
 PLANE_ROWS = 4
 QUADRANTS = 4
+GATE_BLOCKS = 2 * CHUNKS * BLOCKS
+BLOCKS_PER_ROW_TILE = 5
+BLOCKS_PER_BUNCH = 2
 
 FLOPS = 3 * 2 * BATCH * HIDDEN * SLOTS
 
@@ -58,11 +62,14 @@ def tile_persistentgrucell_pc_kernel(
     out_rows = out.rearrange("(p t) n -> p t n", t=ROW_TILES)
 
     with ExitStack() as stack:
+        stack.enter_context(tc.manual_schedule())
         keep = stack.enter_context(tc.tile_pool(name="keep", bufs=1))
-        gate_pool = stack.enter_context(tc.tile_pool(name="gate", bufs=3))
-        term_pool = stack.enter_context(tc.tile_pool(name="term", bufs=4))
-        acc_pool = stack.enter_context(tc.psum_pool(name="acc", bufs=4))
-        turn_pool = stack.enter_context(tc.psum_pool(name="turn", bufs=4))
+        gate_pool = stack.enter_context(tc.tile_pool(name="gate", bufs=5))
+        term_pool = stack.enter_context(tc.tile_pool(name="term", bufs=8))
+        psum = stack.enter_context(tc.psum_pool(name="psum", bufs=PSUM_BANKS))
+
+        def bank():
+            return psum.tile([P, BANK], F32, name="bank", tag="bank")
 
         hidden_sb = keep.tile([P, ROW_TILES, HIDDEN], BF16)
         grouped = keep.tile([P, PASSES, BATCH, PACK], BF16, align_bytes=64)
@@ -75,26 +82,27 @@ def tile_persistentgrucell_pc_kernel(
         planes_w = keep.tile([P, SLOTS], U8, align_bytes=64)
         memory_sb = keep.tile([P, ROW_TILES, SLOTS], BF16)
         addr = keep.tile([P, ROW_TILES, SLOTS], F32)
-        result = keep.tile([P, ROW_TILES, SLOTS], F32)
         identity = keep.tile([P, P], F32)
         ones = keep.tile([P, P], BF16)
         baddr_row = keep.tile([P, SLOTS], BF16)
         baddr_all = keep.tile([P, SLOTS], F32)
         gate_bias_rows = keep.tile([P, P], BF16)
         gate_bias_rows_f32 = keep.tile([P, P], F32)
-        half_gate_bias = keep.tile([P, 2 * CHUNKS * BLOCKS], F32)
+        half_gate_bias = keep.tile([P, GATE_BLOCKS], F32)
         scaled_hidden = keep.tile([P, ROW_TILES, HIDDEN], BF16)
+        table_warm = keep.tile([P, 1], F32)
         half_mean = keep.tile([P, ROW_TILES], F32)
         neg_max = keep.tile([P, ROW_TILES], F32)
         exp_sum = keep.tile([P, ROW_TILES], F32)
         inv_sum = keep.tile([P, ROW_TILES], F32)
 
+        nc.vector.memset(ones[:], 1.0)
+        nc.vector.memset(baddr_row[:], 0.0)
+        nc.vector.memset(gate_bias_rows[:], 0.0)
         nc.vector.memset(planes_af[:].bitcast(I32), 0)
         nc.vector.memset(planes_w[:].bitcast(I32), 0)
-        nc.vector.memset(gate_bias_rows[:], 0.0)
-        nc.vector.memset(baddr_row[:], 0.0)
-        nc.vector.memset(ones[:], 1.0)
         make_identity(nc, identity[:])
+        nc.scalar.activation(out=table_warm[:], in_=ones[:, 0:1], func=ACT.Tanh)
 
         def load_words(dst, words, c):
             view = words.rearrange("g p n j -> g p (n j)").bitcast(I32).rearrange("g p n -> p g n")
@@ -109,11 +117,11 @@ def tile_persistentgrucell_pc_kernel(
                     in_=rows[:, PLANE_ROWS * quadrant : PLANE_ROWS * (quadrant + 1), :],
                 )
 
-        for t in range(ROW_TILES):
-            nc.sync.dma_start(out=hidden_sb[:, t, :], in_=hidden_rows[:, t, :])
         nc.scalar.dma_start(out=baddr_row[0:1, :], in_=baddr.rearrange("(o n) -> o n", o=1))
         nc.scalar.dma_start(out=gate_bias_rows[0:16, :], in_=bforget.rearrange("(i p) -> i p", p=P))
         nc.scalar.dma_start(out=gate_bias_rows[16:32, :], in_=bwrite.rearrange("(i p) -> i p", p=P))
+        for t in range(ROW_TILES):
+            nc.sync.dma_start(out=hidden_sb[:, t, :], in_=hidden_rows[:, t, :])
         load_scales(planes_af, 0, Waddr_scales)
         for c in range(CHUNKS):
             load_words(wa_words, Waddr_words, c)
@@ -121,24 +129,23 @@ def tile_persistentgrucell_pc_kernel(
         load_scales(planes_w, 0, Wwrite_scales)
         for c in range(CHUNKS):
             load_words(wf_words, Wforget_words, c)
-            nc.sync.dma_start(out=memory_sb[:, :, chunk_cols(c)], in_=memory_rows[:, :, chunk_cols(c)])
-        for c in range(CHUNKS):
             load_words(ww_words, Wwrite_words, c)
+            nc.sync.dma_start(out=memory_sb[:, :, chunk_cols(c)], in_=memory_rows[:, :, chunk_cols(c)])
 
         for c in range(CHUNKS):
-            spread = acc_pool.tile([P, BANK], F32, tag="acc")
+            spread = bank()
             nc.tensor.matmul(out=spread[:], lhsT=ones[:], rhs=baddr_row[:, chunk_cols(c)], start=True, stop=True)
             nc.vector.tensor_copy(out=baddr_all[:, chunk_cols(c)], in_=spread[:])
         nc.vector.tensor_copy(out=gate_bias_rows_f32[:], in_=gate_bias_rows[:])
-        bias_cols = turn_pool.tile([P, BANK], F32, tag="turn")
+        bias_cols = bank()
         nc.tensor.transpose(bias_cols[:, 0:P], gate_bias_rows_f32[:], identity[:])
-        nc.vector.tensor_scalar_mul(out=half_gate_bias[:], in0=bias_cols[:, 0 : 2 * CHUNKS * BLOCKS], scalar1=0.5)
+        nc.vector.tensor_scalar_mul(out=half_gate_bias[:], in0=bias_cols[:, 0:GATE_BLOCKS], scalar1=0.5)
 
         hidden_words = hidden_sb[:].bitcast(F32)
         grouped_words = grouped[:].bitcast(F32)
         words_per_pass = K_PASS // 2
         for t in range(ROW_TILES):
-            turned = turn_pool.tile([P, BANK], F32, tag="turn")
+            turned = bank()
             for g in range(PASSES):
                 for u in range(2):
                     nc.tensor.transpose(
@@ -165,26 +172,29 @@ def tile_persistentgrucell_pc_kernel(
                 accum_out=half_mean[:, t : t + 1],
             )
 
-        def addr_scores(t, c):
-            acc = acc_pool.tile([P, BANK], F32, tag="acc")
-            for g in range(PASSES):
-                nc.tensor.matmul_mx(
-                    out=acc[:],
-                    lhsT=h_codes[:, g, block_cols(t)].bitcast(FP8X4),
-                    lhsT_scale=h_scales[:, g, block_cols(t)],
-                    rhs=wa_words[:, g, chunk_cols(c)].bitcast(FP8X4),
-                    rhs_scale=planes_af[PLANE_ROWS * g : P, chunk_cols(c)],
-                    start=(g == 0),
-                    stop=(g == PASSES - 1),
+        def addr_scores(t):
+            for c in range(CHUNKS):
+                acc = bank()
+                for g in range(PASSES):
+                    nc.tensor.matmul_mx(
+                        out=acc[:],
+                        lhsT=h_codes[:, g, block_cols(t)].bitcast(FP8X4),
+                        lhsT_scale=h_scales[:, g, block_cols(t)],
+                        rhs=wa_words[:, g, chunk_cols(c)].bitcast(FP8X4),
+                        rhs_scale=planes_af[PLANE_ROWS * g : P, chunk_cols(c)],
+                        start=(g == 0),
+                        stop=(g == PASSES - 1),
+                    )
+                nc.vector.tensor_tensor(
+                    out=addr[:, t, chunk_cols(c)], in0=acc[:], in1=baddr_all[:, chunk_cols(c)], op=ALU.add
                 )
-            nc.vector.tensor_tensor(
-                out=addr[:, t, chunk_cols(c)], in0=acc[:], in1=baddr_all[:, chunk_cols(c)], op=ALU.add
-            )
 
-        def addr_softmax(t):
+        def softmax_max(t):
             nc.vector.tensor_reduce(
                 out=neg_max[:, t : t + 1], in_=addr[:, t, :], axis=mybir.AxisListType.X, op=ALU.max, negate=True
             )
+
+        def softmax_exp(t):
             nc.scalar.activation(
                 out=addr[:, t, :],
                 in_=addr[:, t, :],
@@ -193,6 +203,8 @@ def tile_persistentgrucell_pc_kernel(
                 scale=1.0,
                 accum_out=exp_sum[:, t : t + 1],
             )
+
+        def softmax_scale(t):
             nc.vector.reciprocal(out=inv_sum[:, t : t + 1], in_=exp_sum[:, t : t + 1])
             nc.gpsimd.tensor_scalar(
                 out=addr[:, t, :],
@@ -203,11 +215,28 @@ def tile_persistentgrucell_pc_kernel(
                 op1=ALU.mult,
             )
 
-        def gate_tanh(words, planes, first_row, first_bias, c):
-            gate_t = gate_pool.tile([P, BLOCKS, BATCH], F32, tag="gate_t")
-            for i in range(BLOCKS):
+        def halve_memory(c):
+            nc.gpsimd.tensor_scalar(
+                out=memory_sb[:, :, chunk_cols(c)],
+                in0=memory_sb[:, :, chunk_cols(c)],
+                scalar1=0.5,
+                scalar2=0.0,
+                op0=ALU.mult,
+                op1=ALU.add,
+            )
+
+        gate_tanh = {}
+        gate_operands = {"forget": (wf_words, planes_af, 8, 0), "write": (ww_words, planes_w, 0, CHUNKS * BLOCKS)}
+        issued = [0]
+
+        def gate_blocks(count):
+            for n in range(issued[0], min(issued[0] + count, GATE_BLOCKS)):
+                c, gate, i = n // (2 * BLOCKS), ("forget", "write")[n // BLOCKS % 2], n % BLOCKS
+                words, planes, first_row, first_bias = gate_operands[gate]
+                if i == 0:
+                    gate_tanh[(gate, c)] = gate_pool.tile([P, BLOCKS, BATCH], F32, name="gate_t", tag="gate_t")
                 block = BLOCKS * c + i
-                acc = acc_pool.tile([P, BANK], F32, tag="acc")
+                acc = bank()
                 for g in range(PASSES):
                     nc.tensor.matmul_mx(
                         out=acc[:],
@@ -219,64 +248,55 @@ def tile_persistentgrucell_pc_kernel(
                         stop=(g == PASSES - 1),
                     )
                 nc.scalar.activation(
-                    out=gate_t[:, i, :],
+                    out=gate_tanh[(gate, c)][:, i, :],
                     in_=acc[:],
                     func=ACT.Tanh,
                     bias=half_gate_bias[:, first_bias + block : first_bias + block + 1],
                     scale=0.5,
                 )
-            return gate_t
+            issued[0] = min(issued[0] + count, GATE_BLOCKS)
 
-        def turn_back(gate_t, t):
-            turned = turn_pool.tile([P, BANK], F32, tag="turn")
-            for i in range(BLOCKS):
-                nc.tensor.transpose(turned[:, block_cols(i)], gate_t[:, i, block_cols(t)], identity[:])
-            return turned
-
-        def forget_term(gate_t, c):
+        def turn_back(gate, c):
+            banks = []
             for t in range(ROW_TILES):
-                turned = turn_back(gate_t, t)
-                nc.vector.scalar_tensor_tensor(
-                    out=result[:, t, chunk_cols(c)],
-                    in0=turned[:],
-                    scalar=1.0,
-                    in1=memory_sb[:, t, chunk_cols(c)],
-                    op0=ALU.add,
-                    op1=ALU.mult,
-                )
+                turned = bank()
+                for i in range(BLOCKS):
+                    nc.tensor.transpose(turned[:, block_cols(i)], gate_tanh[(gate, c)][:, i, block_cols(t)], identity[:])
+                banks.append(turned)
+            return banks
 
-        def write_term_and_store(gate_t, c):
+        def one_plus_times(dst, turned, factor):
+            nc.vector.scalar_tensor_tensor(out=dst, in0=turned[:], scalar=1.0, in1=factor, op0=ALU.add, op1=ALU.mult)
+
+        def forget_terms(c):
+            banks = turn_back("forget", c)
+            gate_blocks(BLOCKS_PER_BUNCH)
+            terms = []
             for t in range(ROW_TILES):
-                turned = turn_back(gate_t, t)
-                term = term_pool.tile([P, BANK], F32, tag="term")
-                nc.vector.scalar_tensor_tensor(
-                    out=term[:],
-                    in0=turned[:],
-                    scalar=1.0,
-                    in1=addr[:, t, chunk_cols(c)],
-                    op0=ALU.add,
-                    op1=ALU.mult,
-                )
-                nc.gpsimd.tensor_tensor(
-                    out=result[:, t, chunk_cols(c)], in0=term[:], in1=result[:, t, chunk_cols(c)], op=ALU.add
-                )
-                nc.sync.dma_start(out=out_rows[:, t, chunk_cols(c)], in_=result[:, t, chunk_cols(c)])
+                term = term_pool.tile([P, BANK], F32, name="forget_term", tag="forget_term")
+                one_plus_times(term[:], banks[t], memory_sb[:, t, chunk_cols(c)])
+                terms.append(term)
+            return terms
 
-        for pair in range(ROW_TILES // 2):
-            for c in range(CHUNKS):
-                for t in (2 * pair, 2 * pair + 1):
-                    addr_scores(t, c)
-            for t in (2 * pair, 2 * pair + 1):
-                addr_softmax(t)
-            for c in (2 * pair, 2 * pair + 1):
-                nc.gpsimd.tensor_scalar(
-                    out=memory_sb[:, :, chunk_cols(c)],
-                    in0=memory_sb[:, :, chunk_cols(c)],
-                    scalar1=0.5,
-                    scalar2=0.0,
-                    op0=ALU.mult,
-                    op1=ALU.add,
-                )
-                forget_term(gate_tanh(wf_words, planes_af, 8, 0, c), c)
+        def write_terms_and_store(c, forget_term):
+            banks = turn_back("write", c)
+            gate_blocks(BLOCKS_PER_BUNCH)
+            for t in range(ROW_TILES):
+                total = term_pool.tile([P, BANK], F32, name="total", tag="total")
+                one_plus_times(total[:], banks[t], addr[:, t, chunk_cols(c)])
+                nc.gpsimd.tensor_tensor(out=total[:], in0=total[:], in1=forget_term[t][:], op=ALU.add)
+                nc.sync.dma_start(out=out_rows[:, t, chunk_cols(c)], in_=total[:])
+
+        for t in range(ROW_TILES):
+            addr_scores(t)
+            if t > 0:
+                softmax_scale(t - 1)
+            softmax_max(t)
+            gate_blocks(BLOCKS_PER_ROW_TILE)
+            softmax_exp(t)
+            halve_memory(t)
         for c in range(CHUNKS):
-            write_term_and_store(gate_tanh(ww_words, planes_w, 0, CHUNKS * BLOCKS, c), c)
+            forget_term = forget_terms(c)
+            if c == 0:
+                softmax_scale(ROW_TILES - 1)
+            write_terms_and_store(c, forget_term)

@@ -123,12 +123,16 @@ def tile_persistentgrucell_pc_kernel(
         for t in range(ROW_TILES):
             nc.sync.dma_start(out=hidden_sb[:, t, :], in_=hidden_rows[:, t, :])
         load_scales(planes_af, 0, Waddr_scales)
-        for c in range(CHUNKS):
-            load_words(wa_words, Waddr_words, c)
+        load_words(wa_words, Waddr_words, 0)
+        load_words(wa_words, Waddr_words, 1)
         load_scales(planes_af, 8, Wforget_scales)
+        load_words(wa_words, Waddr_words, 2)
+        load_words(wa_words, Waddr_words, 3)
+        load_words(wf_words, Wforget_words, 0)
         load_scales(planes_w, 0, Wwrite_scales)
         for c in range(CHUNKS):
-            load_words(wf_words, Wforget_words, c)
+            if c > 0:
+                load_words(wf_words, Wforget_words, c)
             load_words(ww_words, Wwrite_words, c)
             nc.sync.dma_start(out=memory_sb[:, :, chunk_cols(c)], in_=memory_rows[:, :, chunk_cols(c)])
 
@@ -172,7 +176,8 @@ def tile_persistentgrucell_pc_kernel(
                 accum_out=half_mean[:, t : t + 1],
             )
 
-        def addr_scores(t):
+        def addr_passes(t):
+            banks = []
             for c in range(CHUNKS):
                 acc = bank()
                 for g in range(PASSES):
@@ -185,8 +190,13 @@ def tile_persistentgrucell_pc_kernel(
                         start=(g == 0),
                         stop=(g == PASSES - 1),
                     )
+                banks.append(acc)
+            return banks
+
+        def addr_bias(t, banks):
+            for c in range(CHUNKS):
                 nc.vector.tensor_tensor(
-                    out=addr[:, t, chunk_cols(c)], in0=acc[:], in1=baddr_all[:, chunk_cols(c)], op=ALU.add
+                    out=addr[:, t, chunk_cols(c)], in0=banks[c][:], in1=baddr_all[:, chunk_cols(c)], op=ALU.add
                 )
 
         def softmax_max(t):
@@ -287,14 +297,16 @@ def tile_persistentgrucell_pc_kernel(
                 nc.gpsimd.tensor_tensor(out=total[:], in0=total[:], in1=forget_term[t][:], op=ALU.add)
                 nc.sync.dma_start(out=out_rows[:, t, chunk_cols(c)], in_=total[:])
 
+        addr_bias(0, addr_passes(0))
         for t in range(ROW_TILES):
-            addr_scores(t)
-            if t > 0:
-                softmax_scale(t - 1)
+            next_banks = addr_passes(t + 1) if t + 1 < ROW_TILES else None
             softmax_max(t)
-            gate_blocks(BLOCKS_PER_ROW_TILE)
             softmax_exp(t)
+            gate_blocks(BLOCKS_PER_ROW_TILE)
             halve_memory(t)
+            if t + 1 < ROW_TILES:
+                addr_bias(t + 1, next_banks)
+                softmax_scale(t)
         for c in range(CHUNKS):
             forget_term = forget_terms(c)
             if c == 0:

@@ -64,8 +64,8 @@ def tile_persistentgrucell_pc_kernel(
     with ExitStack() as stack:
         stack.enter_context(tc.manual_schedule())
         keep = stack.enter_context(tc.tile_pool(name="keep", bufs=1))
-        gate_pool = stack.enter_context(tc.tile_pool(name="gate", bufs=5))
-        term_pool = stack.enter_context(tc.tile_pool(name="term", bufs=8))
+        gate_pool = stack.enter_context(tc.tile_pool(name="gate", bufs=6))
+        term_pool = stack.enter_context(tc.tile_pool(name="term", bufs=6))
         psum = stack.enter_context(tc.psum_pool(name="psum", bufs=PSUM_BANKS))
 
         def bank():
@@ -214,9 +214,9 @@ def tile_persistentgrucell_pc_kernel(
                 accum_out=exp_sum[:, t : t + 1],
             )
 
-        def softmax_scale(t):
+        def softmax_scale(t, engine):
             nc.vector.reciprocal(out=inv_sum[:, t : t + 1], in_=exp_sum[:, t : t + 1])
-            nc.gpsimd.tensor_scalar(
+            engine.tensor_scalar(
                 out=addr[:, t, :],
                 in0=addr[:, t, :],
                 scalar1=inv_sum[:, t : t + 1],
@@ -266,35 +266,27 @@ def tile_persistentgrucell_pc_kernel(
                 )
             issued[0] = min(issued[0] + count, GATE_BLOCKS)
 
-        def turn_back(gate, c):
-            banks = []
-            for t in range(ROW_TILES):
-                turned = bank()
-                for i in range(BLOCKS):
-                    nc.tensor.transpose(turned[:, block_cols(i)], gate_tanh[(gate, c)][:, i, block_cols(t)], identity[:])
-                banks.append(turned)
-            return banks
+        def turn_back(gate, c, t):
+            turned = bank()
+            for i in range(BLOCKS):
+                nc.tensor.transpose(turned[:, block_cols(i)], gate_tanh[(gate, c)][:, i, block_cols(t)], identity[:])
+            return turned
 
         def one_plus_times(dst, turned, factor):
             nc.vector.scalar_tensor_tensor(out=dst, in0=turned[:], scalar=1.0, in1=factor, op0=ALU.add, op1=ALU.mult)
 
-        def forget_terms(c):
-            banks = turn_back("forget", c)
+        def products(c, row_tiles):
+            turned = {}
+            for t in row_tiles:
+                for gate in ("forget", "write"):
+                    turned[(gate, t)] = turn_back(gate, c, t)
             gate_blocks(BLOCKS_PER_BUNCH)
-            terms = []
-            for t in range(ROW_TILES):
-                term = term_pool.tile([P, BANK], F32, name="forget_term", tag="forget_term")
-                one_plus_times(term[:], banks[t], memory_sb[:, t, chunk_cols(c)])
-                terms.append(term)
-            return terms
-
-        def write_terms_and_store(c, forget_term):
-            banks = turn_back("write", c)
-            gate_blocks(BLOCKS_PER_BUNCH)
-            for t in range(ROW_TILES):
+            for t in row_tiles:
+                forget_term = term_pool.tile([P, BANK], F32, name="forget_term", tag="forget_term")
                 total = term_pool.tile([P, BANK], F32, name="total", tag="total")
-                one_plus_times(total[:], banks[t], addr[:, t, chunk_cols(c)])
-                nc.gpsimd.tensor_tensor(out=total[:], in0=total[:], in1=forget_term[t][:], op=ALU.add)
+                one_plus_times(forget_term[:], turned[("forget", t)], memory_sb[:, t, chunk_cols(c)])
+                one_plus_times(total[:], turned[("write", t)], addr[:, t, chunk_cols(c)])
+                nc.gpsimd.tensor_tensor(out=total[:], in0=total[:], in1=forget_term[:], op=ALU.add)
                 nc.sync.dma_start(out=out_rows[:, t, chunk_cols(c)], in_=total[:])
 
         addr_bias(0, addr_passes(0))
@@ -306,9 +298,9 @@ def tile_persistentgrucell_pc_kernel(
             halve_memory(t)
             if t + 1 < ROW_TILES:
                 addr_bias(t + 1, next_banks)
-                softmax_scale(t)
+                softmax_scale(t, nc.gpsimd)
         for c in range(CHUNKS):
-            forget_term = forget_terms(c)
+            products(c, (0, 1))
             if c == 0:
-                softmax_scale(ROW_TILES - 1)
-            write_terms_and_store(c, forget_term)
+                softmax_scale(ROW_TILES - 1, nc.vector)
+            products(c, (2, 3))

@@ -78,14 +78,15 @@ def tile_persistentgrucell_pc_kernel(
         wa_words = keep.tile([P, PASSES, SLOTS], U32, align_bytes=64)
         wf_words = keep.tile([P, PASSES, SLOTS], U32, align_bytes=64)
         ww_words = keep.tile([P, PASSES, SLOTS], U32, align_bytes=64)
-        planes_af = keep.tile([P, SLOTS], U8, align_bytes=64)
+        planes_a = keep.tile([P, SLOTS], U8, align_bytes=64)
+        planes_f = keep.tile([P, SLOTS], U8, align_bytes=64)
         planes_w = keep.tile([P, SLOTS], U8, align_bytes=64)
         memory_sb = keep.tile([P, ROW_TILES, SLOTS], BF16)
         addr = keep.tile([P, ROW_TILES, SLOTS], F32)
         identity = keep.tile([P, P], F32)
         ones = keep.tile([P, P], BF16)
         baddr_row = keep.tile([P, SLOTS], BF16)
-        baddr_all = keep.tile([P, SLOTS], F32)
+        baddr_all = keep.tile([P, SLOTS], BF16)
         gate_bias_rows = keep.tile([P, P], BF16)
         gate_bias_rows_f32 = keep.tile([P, P], F32)
         half_gate_bias = keep.tile([P, GATE_BLOCKS], F32)
@@ -96,59 +97,57 @@ def tile_persistentgrucell_pc_kernel(
         exp_sum = keep.tile([P, ROW_TILES], F32)
         inv_sum = keep.tile([P, ROW_TILES], F32)
 
+        nc.vector.memset(baddr_row[:].bitcast(I32), 0)
+        nc.vector.memset(gate_bias_rows[:].bitcast(I32), 0)
         nc.vector.memset(ones[:], 1.0)
-        nc.vector.memset(baddr_row[:], 0.0)
-        nc.vector.memset(gate_bias_rows[:], 0.0)
-        nc.vector.memset(planes_af[:].bitcast(I32), 0)
+        nc.vector.memset(planes_a[:].bitcast(I32), 0)
+        nc.vector.memset(planes_f[:].bitcast(I32), 0)
         nc.vector.memset(planes_w[:].bitcast(I32), 0)
         make_identity(nc, identity[:])
-        nc.scalar.activation(out=table_warm[:], in_=ones[:, 0:1], func=ACT.Tanh)
 
         def load_words(dst, words, c):
             view = words.rearrange("g p n j -> g p (n j)").bitcast(I32).rearrange("g p n -> p g n")
             nc.sync.dma_start(out=dst[:, :, chunk_cols(c)].bitcast(I32), in_=view[:, :, chunk_cols(c)])
 
-        def load_scales(planes, first_row, scales):
+        def load_scales(planes, scales):
             rows = scales.bitcast(I32)
             for quadrant in range(QUADRANTS):
-                start = 32 * quadrant + first_row
+                start = 32 * quadrant
                 nc.sync.dma_start(
                     out=planes[start : start + PASSES * PLANE_ROWS, :].bitcast(I32),
                     in_=rows[:, PLANE_ROWS * quadrant : PLANE_ROWS * (quadrant + 1), :],
                 )
 
+        def load_hidden(t):
+            nc.sync.dma_start(out=hidden_sb[:, t, :], in_=hidden_rows[:, t, :])
+
         nc.scalar.dma_start(out=baddr_row[0:1, :], in_=baddr.rearrange("(o n) -> o n", o=1))
         nc.scalar.dma_start(out=gate_bias_rows[0:16, :], in_=bforget.rearrange("(i p) -> i p", p=P))
         nc.scalar.dma_start(out=gate_bias_rows[16:32, :], in_=bwrite.rearrange("(i p) -> i p", p=P))
-        for t in range(ROW_TILES):
-            nc.sync.dma_start(out=hidden_sb[:, t, :], in_=hidden_rows[:, t, :])
-        load_scales(planes_af, 0, Waddr_scales)
+        nc.scalar.activation(out=table_warm[:], in_=identity[:, 0:1], func=ACT.Tanh)
+        load_hidden(0)
+        load_hidden(1)
+        load_scales(planes_a, Waddr_scales)
         load_words(wa_words, Waddr_words, 0)
         load_words(wa_words, Waddr_words, 1)
-        load_scales(planes_af, 8, Wforget_scales)
         load_words(wa_words, Waddr_words, 2)
+        load_hidden(2)
+        load_hidden(3)
         load_words(wa_words, Waddr_words, 3)
+        load_scales(planes_f, Wforget_scales)
         load_words(wf_words, Wforget_words, 0)
-        load_scales(planes_w, 0, Wwrite_scales)
+        load_scales(planes_w, Wwrite_scales)
         for c in range(CHUNKS):
             if c > 0:
                 load_words(wf_words, Wforget_words, c)
             load_words(ww_words, Wwrite_words, c)
             nc.sync.dma_start(out=memory_sb[:, :, chunk_cols(c)], in_=memory_rows[:, :, chunk_cols(c)])
 
-        for c in range(CHUNKS):
-            spread = bank()
-            nc.tensor.matmul(out=spread[:], lhsT=ones[:], rhs=baddr_row[:, chunk_cols(c)], start=True, stop=True)
-            nc.vector.tensor_copy(out=baddr_all[:, chunk_cols(c)], in_=spread[:])
-        nc.vector.tensor_copy(out=gate_bias_rows_f32[:], in_=gate_bias_rows[:])
-        bias_cols = bank()
-        nc.tensor.transpose(bias_cols[:, 0:P], gate_bias_rows_f32[:], identity[:])
-        nc.vector.tensor_scalar_mul(out=half_gate_bias[:], in0=bias_cols[:, 0:GATE_BLOCKS], scalar1=0.5)
-
         hidden_words = hidden_sb[:].bitcast(F32)
         grouped_words = grouped[:].bitcast(F32)
         words_per_pass = K_PASS // 2
-        for t in range(ROW_TILES):
+
+        def turn_hidden(t):
             turned = bank()
             for g in range(PASSES):
                 for u in range(2):
@@ -161,13 +160,27 @@ def tile_persistentgrucell_pc_kernel(
                 out=grouped_words[:, :, block_cols(t), :],
                 in_=turned[:].rearrange("p (g u r) -> p g r u", g=PASSES, u=2),
             )
+
+        def quantise_hidden(t):
             for g in range(PASSES):
                 nc.vector.quantize_mx(
                     out=h_codes[:, g, block_cols(t)].bitcast(FP8X4),
                     scales=h_scales[:, g, block_cols(t)],
                     in_=grouped[:, g, block_cols(t), :].rearrange("p r j -> p (r j)"),
                 )
-        for t in range(ROW_TILES):
+
+        def spread_baddr(c):
+            spread = bank()
+            nc.tensor.matmul(out=spread[:], lhsT=ones[:], rhs=baddr_row[:, chunk_cols(c)], start=True, stop=True)
+            nc.scalar.copy(out=baddr_all[:, chunk_cols(c)], in_=spread[:])
+
+        def gate_biases():
+            nc.vector.tensor_copy(out=gate_bias_rows_f32[:], in_=gate_bias_rows[:])
+            bias_cols = bank()
+            nc.tensor.transpose(bias_cols[:, 0:P], gate_bias_rows_f32[:], identity[:])
+            nc.vector.tensor_scalar_mul(out=half_gate_bias[:], in0=bias_cols[:, 0:GATE_BLOCKS], scalar1=0.5)
+
+        def row_mean(t):
             nc.scalar.activation(
                 out=scaled_hidden[:, t, :],
                 in_=hidden_sb[:, t, :],
@@ -176,9 +189,10 @@ def tile_persistentgrucell_pc_kernel(
                 accum_out=half_mean[:, t : t + 1],
             )
 
-        def addr_passes(t):
+
+        def addr_passes(t, chunks=range(CHUNKS)):
             banks = []
-            for c in range(CHUNKS):
+            for c in chunks:
                 acc = bank()
                 for g in range(PASSES):
                     nc.tensor.matmul_mx(
@@ -186,17 +200,17 @@ def tile_persistentgrucell_pc_kernel(
                         lhsT=h_codes[:, g, block_cols(t)].bitcast(FP8X4),
                         lhsT_scale=h_scales[:, g, block_cols(t)],
                         rhs=wa_words[:, g, chunk_cols(c)].bitcast(FP8X4),
-                        rhs_scale=planes_af[PLANE_ROWS * g : P, chunk_cols(c)],
+                        rhs_scale=planes_a[PLANE_ROWS * g : P, chunk_cols(c)],
                         start=(g == 0),
                         stop=(g == PASSES - 1),
                     )
                 banks.append(acc)
             return banks
 
-        def addr_bias(t, banks):
-            for c in range(CHUNKS):
+        def addr_bias(t, banks, chunks=range(CHUNKS)):
+            for c, acc in zip(chunks, banks):
                 nc.vector.tensor_tensor(
-                    out=addr[:, t, chunk_cols(c)], in0=banks[c][:], in1=baddr_all[:, chunk_cols(c)], op=ALU.add
+                    out=addr[:, t, chunk_cols(c)], in0=acc[:], in1=baddr_all[:, chunk_cols(c)], op=ALU.add
                 )
 
         def softmax_max(t):
@@ -236,7 +250,7 @@ def tile_persistentgrucell_pc_kernel(
             )
 
         gate_tanh = {}
-        gate_operands = {"forget": (wf_words, planes_af, 8, 0), "write": (ww_words, planes_w, 0, CHUNKS * BLOCKS)}
+        gate_operands = {"forget": (wf_words, planes_f, 0, 0), "write": (ww_words, planes_w, 0, CHUNKS * BLOCKS)}
         issued = [0]
 
         def gate_blocks(count):
@@ -275,13 +289,15 @@ def tile_persistentgrucell_pc_kernel(
         def one_plus_times(dst, turned, factor):
             nc.vector.scalar_tensor_tensor(out=dst, in0=turned[:], scalar=1.0, in1=factor, op0=ALU.add, op1=ALU.mult)
 
-        def products(c, row_tiles):
+        def products(c, row_tiles, before_last=None):
             turned = {}
             for t in row_tiles:
                 for gate in ("forget", "write"):
                     turned[(gate, t)] = turn_back(gate, c, t)
             gate_blocks(BLOCKS_PER_BUNCH)
             for t in row_tiles:
+                if before_last is not None and t == row_tiles[-1]:
+                    before_last()
                 forget_term = term_pool.tile([P, BANK], F32, name="forget_term", tag="forget_term")
                 total = term_pool.tile([P, BANK], F32, name="total", tag="total")
                 one_plus_times(forget_term[:], turned[("forget", t)], memory_sb[:, t, chunk_cols(c)])
@@ -289,18 +305,58 @@ def tile_persistentgrucell_pc_kernel(
                 nc.gpsimd.tensor_tensor(out=total[:], in0=total[:], in1=forget_term[:], op=ALU.add)
                 nc.sync.dma_start(out=out_rows[:, t, chunk_cols(c)], in_=total[:])
 
-        addr_bias(0, addr_passes(0))
-        for t in range(ROW_TILES):
-            next_banks = addr_passes(t + 1) if t + 1 < ROW_TILES else None
-            softmax_max(t)
-            softmax_exp(t)
-            gate_blocks(BLOCKS_PER_ROW_TILE)
-            halve_memory(t)
-            if t + 1 < ROW_TILES:
-                addr_bias(t + 1, next_banks)
-                softmax_scale(t, nc.gpsimd)
+        def pair(c):
+            for t in (0, 1):
+                addr_bias(t, addr_passes(t, (c,)), (c,))
+
+        spread_baddr(3)
+        nc.vector.tensor_copy(out=gate_bias_rows_f32[:], in_=gate_bias_rows[:])
+        turn_hidden(0)
+        quantise_hidden(0)
+        spread_baddr(0)
+        turn_hidden(1)
+        quantise_hidden(1)
+        spread_baddr(1)
+        bias_cols = bank()
+        nc.tensor.transpose(bias_cols[:, 0:P], gate_bias_rows_f32[:], identity[:])
+        nc.vector.tensor_scalar_mul(out=half_gate_bias[:], in0=bias_cols[:, 0:GATE_BLOCKS], scalar1=0.5)
+        spread_baddr(2)
+        pair(0)
+        pair(1)
+        row_mean(0)
+        row_mean(1)
+        row_mean(2)
+        pair(2)
+        turn_hidden(2)
+        quantise_hidden(2)
+        turn_hidden(3)
+        quantise_hidden(3)
+        pair(3)
+        row_mean(3)
+        gate_blocks(5)
+        banks2 = addr_passes(2)
+        softmax_max(0)
+        softmax_exp(0)
+        gate_blocks(3)
+        halve_memory(0)
+        softmax_max(1)
+        softmax_exp(1)
+        addr_bias(2, banks2)
+        banks3 = addr_passes(3)
+        gate_blocks(4)
+        halve_memory(1)
+        softmax_scale(0, nc.gpsimd)
+        softmax_max(2)
+        softmax_scale(1, nc.gpsimd)
+        softmax_exp(2)
+        addr_bias(3, banks3)
+        gate_blocks(4)
+        halve_memory(2)
+        softmax_max(3)
+        softmax_scale(2, nc.gpsimd)
+        gate_blocks(4)
+        softmax_exp(3)
+        halve_memory(3)
         for c in range(CHUNKS):
             products(c, (0, 1))
-            if c == 0:
-                softmax_scale(ROW_TILES - 1, nc.vector)
-            products(c, (2, 3))
+            products(c, (2, 3), (lambda: softmax_scale(ROW_TILES - 1, nc.vector)) if c == 0 else None)

@@ -240,7 +240,7 @@ def tile_persistentgrucell_pc_kernel(
             )
 
         def halve_memory(c):
-            nc.gpsimd.tensor_scalar(
+            nc.vector.tensor_scalar(
                 out=memory_sb[:, :, chunk_cols(c)],
                 in0=memory_sb[:, :, chunk_cols(c)],
                 scalar1=0.5,
@@ -338,25 +338,25 @@ def tile_persistentgrucell_pc_kernel(
         softmax_max(0)
         softmax_exp(0)
         gate_blocks(3)
-        halve_memory(0)
         softmax_max(1)
         softmax_exp(1)
         addr_bias(2, banks2)
         banks3 = addr_passes(3)
         gate_blocks(4)
-        halve_memory(1)
         softmax_scale(0, nc.gpsimd)
         softmax_max(2)
         softmax_scale(1, nc.gpsimd)
         softmax_exp(2)
         addr_bias(3, banks3)
         gate_blocks(4)
-        halve_memory(2)
         softmax_max(3)
         softmax_scale(2, nc.gpsimd)
         gate_blocks(4)
         softmax_exp(3)
-        halve_memory(3)
+        halve_memory(0)
+        halve_memory(1)
         for c in range(CHUNKS):
             products(c, (0, 1))
+            if c + 2 < CHUNKS:
+                halve_memory(c + 2)
             products(c, (2, 3), (lambda: softmax_scale(ROW_TILES - 1, nc.vector)) if c == 0 else None)

@@ -302,7 +302,8 @@ def tile_persistentgrucell_pc_kernel(
                 total = term_pool.tile([P, BANK], F32, name="total", tag="total")
                 one_plus_times(forget_term[:], turned[("forget", t)], memory_sb[:, t, chunk_cols(c)])
                 one_plus_times(total[:], turned[("write", t)], addr[:, t, chunk_cols(c)])
-                nc.gpsimd.tensor_tensor(out=total[:], in0=total[:], in1=forget_term[:], op=ALU.add)
+                adder = nc.vector if (c == CHUNKS - 1 and t == ROW_TILES - 1) else nc.gpsimd
+                adder.tensor_tensor(out=total[:], in0=total[:], in1=forget_term[:], op=ALU.add)
                 nc.sync.dma_start(out=out_rows[:, t, chunk_cols(c)], in_=total[:])
 
         def pair(c):

@@ -98,9 +98,9 @@ def tile_persistentgrucell_pc_kernel(
         inv_sum = keep.tile([P, ROW_TILES], F32)
 
         nc.vector.memset(baddr_row[:].bitcast(I32), 0)
+        nc.vector.memset(planes_a[:].bitcast(I32), 0)
         nc.vector.memset(gate_bias_rows[:].bitcast(I32), 0)
         nc.vector.memset(ones[:], 1.0)
-        nc.vector.memset(planes_a[:].bitcast(I32), 0)
         nc.vector.memset(planes_f[:].bitcast(I32), 0)
         nc.vector.memset(planes_w[:].bitcast(I32), 0)
         make_identity(nc, identity[:])
@@ -310,11 +310,11 @@ def tile_persistentgrucell_pc_kernel(
             for t in (0, 1):
                 addr_bias(t, addr_passes(t, (c,)), (c,))
 
-        spread_baddr(3)
         nc.vector.tensor_copy(out=gate_bias_rows_f32[:], in_=gate_bias_rows[:])
         turn_hidden(0)
         quantise_hidden(0)
         spread_baddr(0)
+        spread_baddr(3)
         turn_hidden(1)
         quantise_hidden(1)
         spread_baddr(1)

@@ -121,27 +121,33 @@ def tile_persistentgrucell_pc_kernel(
         def load_hidden(t):
             nc.sync.dma_start(out=hidden_sb[:, t, :], in_=hidden_rows[:, t, :])
 
-        nc.scalar.dma_start(out=baddr_row[0:1, :], in_=baddr.rearrange("(o n) -> o n", o=1))
-        nc.scalar.dma_start(out=gate_bias_rows[0:16, :], in_=bforget.rearrange("(i p) -> i p", p=P))
-        nc.scalar.dma_start(out=gate_bias_rows[16:32, :], in_=bwrite.rearrange("(i p) -> i p", p=P))
         nc.scalar.activation(out=table_warm[:], in_=identity[:, 0:1], func=ACT.Tanh)
         load_hidden(0)
         load_hidden(1)
+        nc.sync.dma_start(out=baddr_row[0:1, :], in_=baddr.rearrange("(o n) -> o n", o=1))
         load_scales(planes_a, Waddr_scales)
         load_words(wa_words, Waddr_words, 0)
         load_words(wa_words, Waddr_words, 1)
         load_words(wa_words, Waddr_words, 2)
+        nc.sync.dma_start(out=gate_bias_rows[0:16, :], in_=bforget.rearrange("(i p) -> i p", p=P))
+        nc.sync.dma_start(out=gate_bias_rows[16:32, :], in_=bwrite.rearrange("(i p) -> i p", p=P))
         load_hidden(2)
         load_hidden(3)
         load_words(wa_words, Waddr_words, 3)
         load_scales(planes_f, Wforget_scales)
         load_words(wf_words, Wforget_words, 0)
         load_scales(planes_w, Wwrite_scales)
-        for c in range(CHUNKS):
-            if c > 0:
-                load_words(wf_words, Wforget_words, c)
-            load_words(ww_words, Wwrite_words, c)
-            nc.sync.dma_start(out=memory_sb[:, :, chunk_cols(c)], in_=memory_rows[:, :, chunk_cols(c)])
+        load_words(ww_words, Wwrite_words, 0)
+        nc.sync.dma_start(out=memory_sb[:, :, chunk_cols(0)], in_=memory_rows[:, :, chunk_cols(0)])
+        load_words(wf_words, Wforget_words, 1)
+        load_words(ww_words, Wwrite_words, 1)
+        nc.sync.dma_start(out=memory_sb[:, :, chunk_cols(1)], in_=memory_rows[:, :, chunk_cols(1)])
+        load_words(wf_words, Wforget_words, 2)
+        load_words(ww_words, Wwrite_words, 2)
+        nc.sync.dma_start(out=memory_sb[:, :, chunk_cols(2)], in_=memory_rows[:, :, chunk_cols(2)])
+        load_words(wf_words, Wforget_words, 3)
+        load_words(ww_words, Wwrite_words, 3)
+        nc.sync.dma_start(out=memory_sb[:, :, chunk_cols(3)], in_=memory_rows[:, :, chunk_cols(3)])
 
         hidden_words = hidden_sb[:].bitcast(F32)
         grouped_words = grouped[:].bitcast(F32)
@@ -310,7 +316,6 @@ def tile_persistentgrucell_pc_kernel(
             for t in (0, 1):
                 addr_bias(t, addr_passes(t, (c,)), (c,))
 
-        nc.vector.tensor_copy(out=gate_bias_rows_f32[:], in_=gate_bias_rows[:])
         turn_hidden(0)
         quantise_hidden(0)
         spread_baddr(0)
@@ -318,12 +323,13 @@ def tile_persistentgrucell_pc_kernel(
         turn_hidden(1)
         quantise_hidden(1)
         spread_baddr(1)
+        spread_baddr(2)
+        pair(0)
+        nc.vector.tensor_copy(out=gate_bias_rows_f32[:], in_=gate_bias_rows[:])
+        pair(1)
         bias_cols = bank()
         nc.tensor.transpose(bias_cols[:, 0:P], gate_bias_rows_f32[:], identity[:])
         nc.vector.tensor_scalar_mul(out=half_gate_bias[:], in0=bias_cols[:, 0:GATE_BLOCKS], scalar1=0.5)
-        spread_baddr(2)
-        pair(0)
-        pair(1)
         row_mean(0)
         row_mean(1)
         row_mean(2)

@@ -318,27 +318,27 @@ def tile_persistentgrucell_pc_kernel(
 
         turn_hidden(0)
         quantise_hidden(0)
-        spread_baddr(0)
-        spread_baddr(3)
         turn_hidden(1)
         quantise_hidden(1)
+        spread_baddr(0)
         spread_baddr(1)
         spread_baddr(2)
+        spread_baddr(3)
         pair(0)
-        nc.vector.tensor_copy(out=gate_bias_rows_f32[:], in_=gate_bias_rows[:])
-        pair(1)
-        bias_cols = bank()
-        nc.tensor.transpose(bias_cols[:, 0:P], gate_bias_rows_f32[:], identity[:])
-        nc.vector.tensor_scalar_mul(out=half_gate_bias[:], in0=bias_cols[:, 0:GATE_BLOCKS], scalar1=0.5)
+        nc.gpsimd.tensor_copy(out=gate_bias_rows_f32[:], in_=gate_bias_rows[:])
         row_mean(0)
         row_mean(1)
-        row_mean(2)
+        pair(1)
         pair(2)
         turn_hidden(2)
         quantise_hidden(2)
         turn_hidden(3)
         quantise_hidden(3)
+        bias_cols = bank()
+        nc.tensor.transpose(bias_cols[:, 0:P], gate_bias_rows_f32[:], identity[:])
+        nc.vector.tensor_scalar_mul(out=half_gate_bias[:], in0=bias_cols[:, 0:GATE_BLOCKS], scalar1=0.5)
         pair(3)
+        row_mean(2)
         row_mean(3)
         gate_blocks(5)
         banks2 = addr_passes(2)

@@ -124,15 +124,14 @@ def tile_persistentgrucell_pc_kernel(
         nc.scalar.activation(out=table_warm[:], in_=identity[:, 0:1], func=ACT.Tanh)
         load_hidden(0)
         load_hidden(1)
+        nc.gpsimd.dma_start(out=gate_bias_rows[0:16, :], in_=bforget.rearrange("(i p) -> i p", p=P))
+        nc.gpsimd.dma_start(out=gate_bias_rows[16:32, :], in_=bwrite.rearrange("(i p) -> i p", p=P))
         nc.sync.dma_start(out=baddr_row[0:1, :], in_=baddr.rearrange("(o n) -> o n", o=1))
         load_scales(planes_a, Waddr_scales)
         load_words(wa_words, Waddr_words, 0)
         load_words(wa_words, Waddr_words, 1)
         load_words(wa_words, Waddr_words, 2)
-        nc.sync.dma_start(out=gate_bias_rows[0:16, :], in_=bforget.rearrange("(i p) -> i p", p=P))
-        nc.sync.dma_start(out=gate_bias_rows[16:32, :], in_=bwrite.rearrange("(i p) -> i p", p=P))
-        load_hidden(2)
-        load_hidden(3)
+        nc.sync.dma_start(out=hidden_sb[:, 2:4, :], in_=hidden_rows[:, 2:4, :])
         load_words(wa_words, Waddr_words, 3)
         load_scales(planes_f, Wforget_scales)
         load_words(wf_words, Wforget_words, 0)

@@ -64,7 +64,7 @@ def tile_persistentgrucell_pc_kernel(
     with ExitStack() as stack:
         stack.enter_context(tc.manual_schedule())
         keep = stack.enter_context(tc.tile_pool(name="keep", bufs=1))
-        gate_pool = stack.enter_context(tc.tile_pool(name="gate", bufs=6))
+        gate_pool = stack.enter_context(tc.tile_pool(name="gate", bufs=8))
         term_pool = stack.enter_context(tc.tile_pool(name="term", bufs=6))
         psum = stack.enter_context(tc.psum_pool(name="psum", bufs=PSUM_BANKS))
 
@@ -244,8 +244,8 @@ def tile_persistentgrucell_pc_kernel(
                 op1=ALU.mult,
             )
 
-        def halve_memory(c):
-            nc.vector.tensor_scalar(
+        def halve_memory(c, engine=nc.vector):
+            engine.tensor_scalar(
                 out=memory_sb[:, :, chunk_cols(c)],
                 in0=memory_sb[:, :, chunk_cols(c)],
                 scalar1=0.5,
@@ -253,6 +253,7 @@ def tile_persistentgrucell_pc_kernel(
                 op0=ALU.mult,
                 op1=ALU.add,
             )
+
 
         gate_tanh = {}
         gate_operands = {"forget": (wf_words, planes_f, 0, 0), "write": (ww_words, planes_w, 0, CHUNKS * BLOCKS)}
@@ -294,12 +295,12 @@ def tile_persistentgrucell_pc_kernel(
         def one_plus_times(dst, turned, factor):
             nc.vector.scalar_tensor_tensor(out=dst, in0=turned[:], scalar=1.0, in1=factor, op0=ALU.add, op1=ALU.mult)
 
-        def products(c, row_tiles, before_last=None):
+        def PR(c, row_tiles, blocks, before_last=None):
             turned = {}
             for t in row_tiles:
                 for gate in ("forget", "write"):
                     turned[(gate, t)] = turn_back(gate, c, t)
-            gate_blocks(BLOCKS_PER_BUNCH)
+            gate_blocks(blocks)
             for t in row_tiles:
                 if before_last is not None and t == row_tiles[-1]:
                     before_last()
@@ -324,7 +325,6 @@ def tile_persistentgrucell_pc_kernel(
         spread_baddr(2)
         spread_baddr(3)
         pair(0)
-        nc.gpsimd.tensor_copy(out=gate_bias_rows_f32[:], in_=gate_bias_rows[:])
         row_mean(0)
         row_mean(1)
         pair(1)
@@ -333,15 +333,16 @@ def tile_persistentgrucell_pc_kernel(
         quantise_hidden(2)
         turn_hidden(3)
         quantise_hidden(3)
+        nc.gpsimd.tensor_copy(out=gate_bias_rows_f32[:], in_=gate_bias_rows[:])
         bias_cols = bank()
         nc.tensor.transpose(bias_cols[:, 0:P], gate_bias_rows_f32[:], identity[:])
         nc.vector.tensor_scalar_mul(out=half_gate_bias[:], in0=bias_cols[:, 0:GATE_BLOCKS], scalar1=0.5)
         pair(3)
         row_mean(2)
         row_mean(3)
-        gate_blocks(5)
-        banks2 = addr_passes(2)
+        gate_blocks(4)
         softmax_max(0)
+        banks2 = addr_passes(2)
         softmax_exp(0)
         gate_blocks(3)
         softmax_max(1)
@@ -352,17 +353,21 @@ def tile_persistentgrucell_pc_kernel(
         softmax_scale(0, nc.gpsimd)
         softmax_max(2)
         softmax_scale(1, nc.gpsimd)
-        softmax_exp(2)
         addr_bias(3, banks3)
+        softmax_exp(2)
         gate_blocks(4)
         softmax_max(3)
         softmax_scale(2, nc.gpsimd)
-        gate_blocks(4)
-        softmax_exp(3)
         halve_memory(0)
+        PR(0, (0, 1), 3)
+        softmax_exp(3)
         halve_memory(1)
-        for c in range(CHUNKS):
-            products(c, (0, 1))
-            if c + 2 < CHUNKS:
-                halve_memory(c + 2)
-            products(c, (2, 3), (lambda: softmax_scale(ROW_TILES - 1, nc.vector)) if c == 0 else None)
+        PR(1, (0, 1), 3)
+        halve_memory(2)
+        PR(0, (2, 3), 3, lambda: softmax_scale(ROW_TILES - 1, nc.vector))
+        PR(1, (2, 3), 3)
+        halve_memory(3)
+        PR(2, (0, 1), 3)
+        PR(2, (2, 3), 2)
+        PR(3, (0, 1), 0)
+        PR(3, (2, 3), 0)

@@ -297,10 +297,10 @@ def tile_persistentgrucell_pc_kernel(
 
         def PR(c, row_tiles, blocks, before_last=None):
             turned = {}
-            for t in row_tiles:
+            for t, count in zip(row_tiles, blocks):
                 for gate in ("forget", "write"):
                     turned[(gate, t)] = turn_back(gate, c, t)
-            gate_blocks(blocks)
+                gate_blocks(count)
             for t in row_tiles:
                 if before_last is not None and t == row_tiles[-1]:
                     before_last()
@@ -359,15 +359,15 @@ def tile_persistentgrucell_pc_kernel(
         softmax_max(3)
         softmax_scale(2, nc.gpsimd)
         halve_memory(0)
-        PR(0, (0, 1), 3)
+        PR(0, (0, 1), (1, 2))
         softmax_exp(3)
         halve_memory(1)
-        PR(1, (0, 1), 3)
+        PR(1, (0, 1), (1, 2))
         halve_memory(2)
-        PR(0, (2, 3), 3, lambda: softmax_scale(ROW_TILES - 1, nc.vector))
-        PR(1, (2, 3), 3)
+        PR(0, (2, 3), (1, 2), lambda: softmax_scale(ROW_TILES - 1, nc.vector))
+        PR(1, (2, 3), (1, 2))
         halve_memory(3)
-        PR(2, (0, 1), 3)
-        PR(2, (2, 3), 2)
-        PR(3, (0, 1), 0)
-        PR(3, (2, 3), 0)
+        PR(2, (0, 1), (1, 2))
+        PR(2, (2, 3), (1, 1))
+        PR(3, (0, 1), (0, 0))
+        PR(3, (2, 3), (0, 0))

@@ -345,6 +345,7 @@ def tile_persistentgrucell_pc_kernel(
         banks2 = addr_passes(2)
         softmax_exp(0)
         gate_blocks(3)
+        halve_memory(0, nc.gpsimd)
         softmax_max(1)
         softmax_exp(1)
         addr_bias(2, banks2)
@@ -358,16 +359,15 @@ def tile_persistentgrucell_pc_kernel(
         gate_blocks(4)
         softmax_max(3)
         softmax_scale(2, nc.gpsimd)
-        halve_memory(0)
         PR(0, (0, 1), (1, 2))
         softmax_exp(3)
         halve_memory(1)
-        PR(1, (0, 1), (1, 2))
+        PR(1, (0, 1), (0, 3))
         halve_memory(2)
-        PR(0, (2, 3), (1, 2), lambda: softmax_scale(ROW_TILES - 1, nc.vector))
-        PR(1, (2, 3), (1, 2))
+        PR(0, (2, 3), (0, 3), lambda: softmax_scale(ROW_TILES - 1, nc.vector))
+        PR(1, (2, 3), (0, 3))
         halve_memory(3)
-        PR(2, (0, 1), (1, 2))
-        PR(2, (2, 3), (1, 1))
+        PR(2, (0, 1), (0, 3))
+        PR(2, (2, 3), (0, 2))
         PR(3, (0, 1), (0, 0))
         PR(3, (2, 3), (0, 0))

@@ -109,13 +109,12 @@ def tile_persistentgrucell_pc_kernel(
             view = words.rearrange("g p n j -> g p (n j)").bitcast(I32).rearrange("g p n -> p g n")
             nc.sync.dma_start(out=dst[:, :, chunk_cols(c)].bitcast(I32), in_=view[:, :, chunk_cols(c)])
 
-        def load_scales(planes, scales):
-            rows = scales.bitcast(I32)
+        def load_scales(planes, scales, cols=slice(0, SLOTS)):
             for quadrant in range(QUADRANTS):
                 start = 32 * quadrant
                 nc.sync.dma_start(
-                    out=planes[start : start + PASSES * PLANE_ROWS, :].bitcast(I32),
-                    in_=rows[:, PLANE_ROWS * quadrant : PLANE_ROWS * (quadrant + 1), :],
+                    out=planes[start : start + PASSES * PLANE_ROWS, cols].bitcast(I32),
+                    in_=scales[:, PLANE_ROWS * quadrant : PLANE_ROWS * (quadrant + 1), cols].bitcast(I32),
                 )
 
         def load_hidden(t):
@@ -133,11 +132,13 @@ def tile_persistentgrucell_pc_kernel(
         load_words(wa_words, Waddr_words, 2)
         nc.sync.dma_start(out=hidden_sb[:, 2:4, :], in_=hidden_rows[:, 2:4, :])
         load_words(wa_words, Waddr_words, 3)
-        load_scales(planes_f, Wforget_scales)
+        load_scales(planes_f, Wforget_scales, chunk_cols(0))
         load_words(wf_words, Wforget_words, 0)
-        load_scales(planes_w, Wwrite_scales)
+        load_scales(planes_w, Wwrite_scales, chunk_cols(0))
         load_words(ww_words, Wwrite_words, 0)
         nc.sync.dma_start(out=memory_sb[:, :, chunk_cols(0)], in_=memory_rows[:, :, chunk_cols(0)])
+        load_scales(planes_f, Wforget_scales, slice(BANK, SLOTS))
+        load_scales(planes_w, Wwrite_scales, slice(BANK, SLOTS))
         load_words(wf_words, Wforget_words, 1)
         load_words(ww_words, Wwrite_words, 1)
         nc.sync.dma_start(out=memory_sb[:, :, chunk_cols(1)], in_=memory_rows[:, :, chunk_cols(1)])
@@ -334,10 +335,10 @@ def tile_persistentgrucell_pc_kernel(
         turn_hidden(3)
         quantise_hidden(3)
         nc.gpsimd.tensor_copy(out=gate_bias_rows_f32[:], in_=gate_bias_rows[:])
+        pair(3)
         bias_cols = bank()
         nc.tensor.transpose(bias_cols[:, 0:P], gate_bias_rows_f32[:], identity[:])
         nc.vector.tensor_scalar_mul(out=half_gate_bias[:], in0=bias_cols[:, 0:GATE_BLOCKS], scalar1=0.5)
-        pair(3)
         row_mean(2)
         row_mean(3)
         gate_blocks(4)

@@ -29,6 +29,7 @@ QUADRANTS = 4
 GATE_BLOCKS = 2 * CHUNKS * BLOCKS
 BLOCKS_PER_ROW_TILE = 5
 BLOCKS_PER_BUNCH = 2
+WARM_UP = 3
 
 FLOPS = 3 * 2 * BATCH * HIDDEN * SLOTS
 
@@ -72,7 +73,7 @@ def tile_persistentgrucell_pc_kernel(
             return psum.tile([P, BANK], F32, name="bank", tag="bank")
 
         hidden_sb = keep.tile([P, ROW_TILES, HIDDEN], BF16)
-        grouped = keep.tile([P, PASSES, BATCH, PACK], BF16, align_bytes=64)
+        grouped = [keep.tile([P, PASSES, P, PACK], BF16, name="grouped%d" % t, align_bytes=64) for t in range(ROW_TILES)]
         h_codes = keep.tile([P, PASSES, BATCH], U32, align_bytes=64)
         h_scales = keep.tile([P, PASSES, BATCH], U8, align_bytes=64)
         wa_words = keep.tile([P, PASSES, SLOTS], U32, align_bytes=64)
@@ -87,6 +88,7 @@ def tile_persistentgrucell_pc_kernel(
         ones = keep.tile([P, P], BF16)
         baddr_row = keep.tile([P, SLOTS], BF16)
         baddr_all = keep.tile([P, SLOTS], BF16)
+        zeros = keep.tile([P, BANK], BF16)
         gate_bias_rows = keep.tile([P, P], BF16)
         gate_bias_rows_f32 = keep.tile([P, P], F32)
         half_gate_bias = keep.tile([P, GATE_BLOCKS], F32)
@@ -97,8 +99,9 @@ def tile_persistentgrucell_pc_kernel(
         exp_sum = keep.tile([P, ROW_TILES], F32)
         inv_sum = keep.tile([P, ROW_TILES], F32)
 
-        nc.vector.memset(baddr_row[:].bitcast(I32), 0)
+        nc.gpsimd.memset(baddr_row[:].bitcast(F32), 0.0)
         nc.vector.memset(planes_a[:].bitcast(I32), 0)
+        nc.vector.memset(zeros[:].bitcast(I32), 0)
         nc.vector.memset(gate_bias_rows[:].bitcast(I32), 0)
         nc.vector.memset(ones[:], 1.0)
         nc.vector.memset(planes_f[:].bitcast(I32), 0)
@@ -120,16 +123,16 @@ def tile_persistentgrucell_pc_kernel(
         def load_hidden(t):
             nc.sync.dma_start(out=hidden_sb[:, t, :], in_=hidden_rows[:, t, :])
 
-        nc.scalar.activation(out=table_warm[:], in_=identity[:, 0:1], func=ACT.Tanh)
+        nc.scalar.activation(out=table_warm[:], in_=ones[:, 0:1], func=ACT.Tanh)
         load_hidden(0)
         load_hidden(1)
-        nc.gpsimd.dma_start(out=gate_bias_rows[0:16, :], in_=bforget.rearrange("(i p) -> i p", p=P))
-        nc.gpsimd.dma_start(out=gate_bias_rows[16:32, :], in_=bwrite.rearrange("(i p) -> i p", p=P))
-        nc.sync.dma_start(out=baddr_row[0:1, :], in_=baddr.rearrange("(o n) -> o n", o=1))
         load_scales(planes_a, Waddr_scales)
+        nc.sync.dma_start(out=baddr_row[0:1, :], in_=baddr.rearrange("(o n) -> o n", o=1))
         load_words(wa_words, Waddr_words, 0)
         load_words(wa_words, Waddr_words, 1)
         load_words(wa_words, Waddr_words, 2)
+        nc.sync.dma_start(out=gate_bias_rows[0:16, :], in_=bforget.rearrange("(i p) -> i p", p=P))
+        nc.sync.dma_start(out=gate_bias_rows[16:32, :], in_=bwrite.rearrange("(i p) -> i p", p=P))
         nc.sync.dma_start(out=hidden_sb[:, 2:4, :], in_=hidden_rows[:, 2:4, :])
         load_words(wa_words, Waddr_words, 3)
         load_scales(planes_f, Wforget_scales, chunk_cols(0))
@@ -150,7 +153,6 @@ def tile_persistentgrucell_pc_kernel(
         nc.sync.dma_start(out=memory_sb[:, :, chunk_cols(3)], in_=memory_rows[:, :, chunk_cols(3)])
 
         hidden_words = hidden_sb[:].bitcast(F32)
-        grouped_words = grouped[:].bitcast(F32)
         words_per_pass = K_PASS // 2
 
         def turn_hidden(t):
@@ -163,7 +165,7 @@ def tile_persistentgrucell_pc_kernel(
                         identity[:],
                     )
             nc.scalar.copy(
-                out=grouped_words[:, :, block_cols(t), :],
+                out=grouped[t][:].bitcast(F32),
                 in_=turned[:].rearrange("p (g u r) -> p g r u", g=PASSES, u=2),
             )
 
@@ -172,7 +174,7 @@ def tile_persistentgrucell_pc_kernel(
                 nc.vector.quantize_mx(
                     out=h_codes[:, g, block_cols(t)].bitcast(FP8X4),
                     scales=h_scales[:, g, block_cols(t)],
-                    in_=grouped[:, g, block_cols(t), :].rearrange("p r j -> p (r j)"),
+                    in_=grouped[t][:, g, :, :].rearrange("p r j -> p (r j)"),
                 )
 
         def spread_baddr(c):
@@ -245,6 +247,9 @@ def tile_persistentgrucell_pc_kernel(
                 op1=ALU.mult,
             )
 
+        def halve_on_scalar(c, ts):
+            nc.scalar.activation(out=memory_sb[:, ts, chunk_cols(c)], in_=memory_sb[:, ts, chunk_cols(c)], func=ACT.Copy, scale=0.5)
+
         def halve_memory(c, engine=nc.vector):
             engine.tensor_scalar(
                 out=memory_sb[:, :, chunk_cols(c)],
@@ -309,14 +314,23 @@ def tile_persistentgrucell_pc_kernel(
                 total = term_pool.tile([P, BANK], F32, name="total", tag="total")
                 one_plus_times(forget_term[:], turned[("forget", t)], memory_sb[:, t, chunk_cols(c)])
                 one_plus_times(total[:], turned[("write", t)], addr[:, t, chunk_cols(c)])
-                adder = nc.vector if (c == CHUNKS - 1 and t == ROW_TILES - 1) else nc.gpsimd
-                adder.tensor_tensor(out=total[:], in0=total[:], in1=forget_term[:], op=ALU.add)
-                nc.sync.dma_start(out=out_rows[:, t, chunk_cols(c)], in_=total[:])
+                last = c == CHUNKS - 1 and t == ROW_TILES - 1
+                adder, pieces = (nc.vector, 2) if last else (nc.gpsimd, 1)
+                width = BANK // pieces
+                for piece in range(pieces):
+                    cols = slice(piece * width, (piece + 1) * width)
+                    adder.tensor_tensor(out=total[:, cols], in0=total[:, cols], in1=forget_term[:, cols], op=ALU.add)
+                    nc.sync.dma_start(
+                        out=out_rows[:, t, c * BANK + piece * width : c * BANK + (piece + 1) * width], in_=total[:, cols]
+                    )
 
         def pair(c):
             for t in (0, 1):
                 addr_bias(t, addr_passes(t, (c,)), (c,))
 
+        warm = bank()
+        for i in range(WARM_UP):
+            nc.tensor.matmul(out=warm[:], lhsT=zeros[:, 0:P], rhs=zeros[:], start=True, stop=True)
         turn_hidden(0)
         quantise_hidden(0)
         turn_hidden(1)
@@ -364,11 +378,13 @@ def tile_persistentgrucell_pc_kernel(
         softmax_exp(3)
         halve_memory(1)
         PR(1, (0, 1), (0, 3))
-        halve_memory(2)
         PR(0, (2, 3), (0, 3), lambda: softmax_scale(ROW_TILES - 1, nc.vector))
+        halve_on_scalar(2, slice(0, 2))
         PR(1, (2, 3), (0, 3))
-        halve_memory(3)
+        halve_on_scalar(2, slice(2, 4))
         PR(2, (0, 1), (0, 3))
+        halve_on_scalar(3, slice(0, 2))
         PR(2, (2, 3), (0, 2))
+        halve_on_scalar(3, slice(2, 4))
         PR(3, (0, 1), (0, 0))
         PR(3, (2, 3), (0, 0))

@@ -85,8 +85,8 @@ def tile_persistentgrucell_pc_kernel(
         memory_sb = keep.tile([P, ROW_TILES, SLOTS], BF16)
         addr = keep.tile([P, ROW_TILES, SLOTS], F32)
         identity = keep.tile([P, P], F32)
-        ones = keep.tile([P, P], BF16)
-        baddr_row = keep.tile([P, SLOTS], BF16)
+        baddr_rows = keep.tile([P, P], BF16)
+        identity_bf16 = keep.tile([P, P], BF16)
         baddr_all = keep.tile([P, SLOTS], BF16)
         zeros = keep.tile([P, BANK], BF16)
         gate_bias_rows = keep.tile([P, P], BF16)
@@ -99,14 +99,14 @@ def tile_persistentgrucell_pc_kernel(
         exp_sum = keep.tile([P, ROW_TILES], F32)
         inv_sum = keep.tile([P, ROW_TILES], F32)
 
-        nc.gpsimd.memset(baddr_row[:].bitcast(F32), 0.0)
+        nc.vector.memset(baddr_rows[:].bitcast(I32), 0)
         nc.vector.memset(planes_a[:].bitcast(I32), 0)
         nc.vector.memset(zeros[:].bitcast(I32), 0)
         nc.vector.memset(gate_bias_rows[:].bitcast(I32), 0)
-        nc.vector.memset(ones[:], 1.0)
         nc.vector.memset(planes_f[:].bitcast(I32), 0)
         nc.vector.memset(planes_w[:].bitcast(I32), 0)
         make_identity(nc, identity[:])
+        nc.vector.tensor_copy(out=identity_bf16[:], in_=identity[:])
 
         def load_words(dst, words, c):
             view = words.rearrange("g p n j -> g p (n j)").bitcast(I32).rearrange("g p n -> p g n")
@@ -123,11 +123,11 @@ def tile_persistentgrucell_pc_kernel(
         def load_hidden(t):
             nc.sync.dma_start(out=hidden_sb[:, t, :], in_=hidden_rows[:, t, :])
 
-        nc.scalar.activation(out=table_warm[:], in_=ones[:, 0:1], func=ACT.Tanh)
+        nc.scalar.activation(out=table_warm[:], in_=zeros[:, 0:1], func=ACT.Tanh)
         load_hidden(0)
         load_hidden(1)
+        nc.sync.dma_start(out=baddr_rows[0:16, :], in_=baddr.rearrange("(i p) -> i p", p=P))
         load_scales(planes_a, Waddr_scales)
-        nc.sync.dma_start(out=baddr_row[0:1, :], in_=baddr.rearrange("(o n) -> o n", o=1))
         load_words(wa_words, Waddr_words, 0)
         load_words(wa_words, Waddr_words, 1)
         load_words(wa_words, Waddr_words, 2)
@@ -141,10 +141,10 @@ def tile_persistentgrucell_pc_kernel(
         load_words(ww_words, Wwrite_words, 0)
         nc.sync.dma_start(out=memory_sb[:, :, chunk_cols(0)], in_=memory_rows[:, :, chunk_cols(0)])
         load_scales(planes_f, Wforget_scales, slice(BANK, SLOTS))
+        nc.sync.dma_start(out=memory_sb[:, :, chunk_cols(1)], in_=memory_rows[:, :, chunk_cols(1)])
         load_scales(planes_w, Wwrite_scales, slice(BANK, SLOTS))
         load_words(wf_words, Wforget_words, 1)
         load_words(ww_words, Wwrite_words, 1)
-        nc.sync.dma_start(out=memory_sb[:, :, chunk_cols(1)], in_=memory_rows[:, :, chunk_cols(1)])
         load_words(wf_words, Wforget_words, 2)
         load_words(ww_words, Wwrite_words, 2)
         nc.sync.dma_start(out=memory_sb[:, :, chunk_cols(2)], in_=memory_rows[:, :, chunk_cols(2)])
@@ -179,14 +179,27 @@ def tile_persistentgrucell_pc_kernel(
 
         def spread_baddr(c):
             spread = bank()
-            nc.tensor.matmul(out=spread[:], lhsT=ones[:], rhs=baddr_row[:, chunk_cols(c)], start=True, stop=True)
+            for i in range(BLOCKS):
+                block = BLOCKS * c + i
+                nc.tensor.matmul(
+                    out=spread[:, block_cols(i)],
+                    lhsT=identity_bf16[:, block : block + 1].to_broadcast([P, P]),
+                    rhs=baddr_rows[:],
+                    start=True,
+                    stop=True,
+                )
             nc.scalar.copy(out=baddr_all[:, chunk_cols(c)], in_=spread[:])
 
-        def gate_biases():
-            nc.vector.tensor_copy(out=gate_bias_rows_f32[:], in_=gate_bias_rows[:])
-            bias_cols = bank()
-            nc.tensor.transpose(bias_cols[:, 0:P], gate_bias_rows_f32[:], identity[:])
-            nc.vector.tensor_scalar_mul(out=half_gate_bias[:], in0=bias_cols[:, 0:GATE_BLOCKS], scalar1=0.5)
+        def row_mean_on_vector(t):
+            nc.vector.tensor_scalar(
+                out=scaled_hidden[:, t, :],
+                in0=hidden_sb[:, t, :],
+                scalar1=0.5 / HIDDEN,
+                scalar2=None,
+                op0=ALU.mult,
+                op1=ALU.add,
+                accum_out=half_mean[:, t : t + 1],
+            )
 
         def row_mean(t):
             nc.scalar.activation(
@@ -349,35 +362,36 @@ def tile_persistentgrucell_pc_kernel(
         turn_hidden(3)
         quantise_hidden(3)
         nc.gpsimd.tensor_copy(out=gate_bias_rows_f32[:], in_=gate_bias_rows[:])
-        pair(3)
         bias_cols = bank()
         nc.tensor.transpose(bias_cols[:, 0:P], gate_bias_rows_f32[:], identity[:])
         nc.vector.tensor_scalar_mul(out=half_gate_bias[:], in0=bias_cols[:, 0:GATE_BLOCKS], scalar1=0.5)
+        pair(3)
         row_mean(2)
-        row_mean(3)
         gate_blocks(4)
         softmax_max(0)
         banks2 = addr_passes(2)
         softmax_exp(0)
         gate_blocks(3)
         halve_memory(0, nc.gpsimd)
+        halve_memory(1, nc.gpsimd)
         softmax_max(1)
         softmax_exp(1)
         addr_bias(2, banks2)
         banks3 = addr_passes(3)
-        gate_blocks(4)
         softmax_scale(0, nc.gpsimd)
         softmax_max(2)
         softmax_scale(1, nc.gpsimd)
-        addr_bias(3, banks3)
+        gate_blocks(1)
         softmax_exp(2)
+        gate_blocks(3)
+        addr_bias(3, banks3)
         gate_blocks(4)
-        softmax_max(3)
         softmax_scale(2, nc.gpsimd)
+        softmax_max(3)
         PR(0, (0, 1), (1, 2))
         softmax_exp(3)
-        halve_memory(1)
         PR(1, (0, 1), (0, 3))
+        row_mean_on_vector(3)
         PR(0, (2, 3), (0, 3), lambda: softmax_scale(ROW_TILES - 1, nc.vector))
         halve_on_scalar(2, slice(0, 2))
         PR(1, (2, 3), (0, 3))

from contextlib import ExitStack

import concourse.mybir as mybir
from concourse.masks import make_identity

F32 = mybir.dt.float32
BF16 = mybir.dt.bfloat16
I32 = mybir.dt.int32
U32 = mybir.dt.uint32
U8 = mybir.dt.uint8
FP8X4 = mybir.dt.float8_e4m3fn_x4
ALU = mybir.AluOpType
ACT = mybir.ActivationFunctionType

P = 128
BATCH = 512
HIDDEN = 1024
SLOTS = 2048
ROW_TILES = BATCH // P
PACK = 4
K_PASS = P * PACK
PASSES = HIDDEN // K_PASS
BANK = 512
PSUM_BANKS = 8
CHUNKS = SLOTS // BANK
BLOCKS = BANK // P
PLANE_ROWS = 4
QUADRANTS = 4
GATE_BLOCKS = 2 * CHUNKS * BLOCKS
BLOCKS_PER_ROW_TILE = 5
BLOCKS_PER_BUNCH = 2
WARM_UP = 3

FLOPS = 3 * 2 * BATCH * HIDDEN * SLOTS


def chunk_cols(c):
    return slice(c * BANK, (c + 1) * BANK)


def block_cols(i):
    return slice(i * P, (i + 1) * P)


def tile_persistentgrucell_pc_kernel(
    tc,
    hidden_new,
    persistent_memory,
    Waddr_words,
    Waddr_scales,
    baddr,
    Wwrite_words,
    Wwrite_scales,
    bwrite,
    Wforget_words,
    Wforget_scales,
    bforget,
    out,
):
    nc = tc.nc
    hidden_rows = hidden_new.rearrange("(p t) k -> p t k", t=ROW_TILES)
    memory_rows = persistent_memory.rearrange("(p t) n -> p t n", t=ROW_TILES)
    out_rows = out.rearrange("(p t) n -> p t n", t=ROW_TILES)

    with ExitStack() as stack:
        stack.enter_context(tc.manual_schedule())
        keep = stack.enter_context(tc.tile_pool(name="keep", bufs=1))
        gate_pool = stack.enter_context(tc.tile_pool(name="gate", bufs=8))
        term_pool = stack.enter_context(tc.tile_pool(name="term", bufs=6))
        psum = stack.enter_context(tc.psum_pool(name="psum", bufs=PSUM_BANKS))

        def bank():
            return psum.tile([P, BANK], F32, name="bank", tag="bank")

        hidden_sb = keep.tile([P, ROW_TILES, HIDDEN], BF16)
        grouped = [keep.tile([P, PASSES, P, PACK], BF16, name="grouped%d" % t, align_bytes=64) for t in range(ROW_TILES)]
        h_codes = keep.tile([P, PASSES, BATCH], U32, align_bytes=64)
        h_scales = keep.tile([P, PASSES, BATCH], U8, align_bytes=64)
        wa_words = keep.tile([P, PASSES, SLOTS], U32, align_bytes=64)
        wf_words = keep.tile([P, PASSES, SLOTS], U32, align_bytes=64)
        ww_words = keep.tile([P, PASSES, SLOTS], U32, align_bytes=64)
        planes_a = keep.tile([P, SLOTS], U8, align_bytes=64)
        planes_f = keep.tile([P, SLOTS], U8, align_bytes=64)
        planes_w = keep.tile([P, SLOTS], U8, align_bytes=64)
        memory_sb = keep.tile([P, ROW_TILES, SLOTS], BF16)
        addr = keep.tile([P, ROW_TILES, SLOTS], F32)
        identity = keep.tile([P, P], F32)
        baddr_rows = keep.tile([P, P], BF16)
        identity_bf16 = keep.tile([P, P], BF16)
        baddr_all = keep.tile([P, SLOTS], BF16)
        zeros = keep.tile([P, BANK], BF16)
        gate_bias_rows = keep.tile([P, P], BF16)
        gate_bias_rows_f32 = keep.tile([P, P], F32)
        half_gate_bias = keep.tile([P, GATE_BLOCKS], F32)
        scaled_hidden = keep.tile([P, ROW_TILES, HIDDEN], BF16)
        table_warm = keep.tile([P, 1], F32)
        half_mean = keep.tile([P, ROW_TILES], F32)
        neg_max = keep.tile([P, ROW_TILES], F32)
        exp_sum = keep.tile([P, ROW_TILES], F32)
        inv_sum = keep.tile([P, ROW_TILES], F32)

        nc.vector.memset(baddr_rows[:].bitcast(I32), 0)
        nc.vector.memset(planes_a[:].bitcast(I32), 0)
        nc.vector.memset(zeros[:].bitcast(I32), 0)
        nc.vector.memset(gate_bias_rows[:].bitcast(I32), 0)
        nc.vector.memset(planes_f[:].bitcast(I32), 0)
        nc.vector.memset(planes_w[:].bitcast(I32), 0)
        make_identity(nc, identity[:])
        nc.vector.tensor_copy(out=identity_bf16[:], in_=identity[:])

        def load_words(dst, words, c):
            view = words.rearrange("g p n j -> g p (n j)").bitcast(I32).rearrange("g p n -> p g n")
            nc.sync.dma_start(out=dst[:, :, chunk_cols(c)].bitcast(I32), in_=view[:, :, chunk_cols(c)])

        def load_scales(planes, scales, cols=slice(0, SLOTS)):
            for quadrant in range(QUADRANTS):
                start = 32 * quadrant
                nc.sync.dma_start(
                    out=planes[start : start + PASSES * PLANE_ROWS, cols].bitcast(I32),
                    in_=scales[:, PLANE_ROWS * quadrant : PLANE_ROWS * (quadrant + 1), cols].bitcast(I32),
                )

        def load_hidden(t):
            nc.sync.dma_start(out=hidden_sb[:, t, :], in_=hidden_rows[:, t, :])

        nc.scalar.activation(out=table_warm[:], in_=zeros[:, 0:1], func=ACT.Tanh)
        load_hidden(0)
        load_hidden(1)
        nc.sync.dma_start(out=baddr_rows[0:16, :], in_=baddr.rearrange("(i p) -> i p", p=P))
        load_scales(planes_a, Waddr_scales)
        load_words(wa_words, Waddr_words, 0)
        load_words(wa_words, Waddr_words, 1)
        load_words(wa_words, Waddr_words, 2)
        nc.sync.dma_start(out=gate_bias_rows[0:16, :], in_=bforget.rearrange("(i p) -> i p", p=P))
        nc.sync.dma_start(out=gate_bias_rows[16:32, :], in_=bwrite.rearrange("(i p) -> i p", p=P))
        nc.sync.dma_start(out=hidden_sb[:, 2:4, :], in_=hidden_rows[:, 2:4, :])
        load_words(wa_words, Waddr_words, 3)
        load_scales(planes_f, Wforget_scales, chunk_cols(0))
        load_words(wf_words, Wforget_words, 0)
        load_scales(planes_w, Wwrite_scales, chunk_cols(0))
        load_words(ww_words, Wwrite_words, 0)
        nc.sync.dma_start(out=memory_sb[:, :, chunk_cols(0)], in_=memory_rows[:, :, chunk_cols(0)])
        load_scales(planes_f, Wforget_scales, slice(BANK, SLOTS))
        nc.sync.dma_start(out=memory_sb[:, :, chunk_cols(1)], in_=memory_rows[:, :, chunk_cols(1)])
        load_scales(planes_w, Wwrite_scales, slice(BANK, SLOTS))
        load_words(wf_words, Wforget_words, 1)
        load_words(ww_words, Wwrite_words, 1)
        load_words(wf_words, Wforget_words, 2)
        load_words(ww_words, Wwrite_words, 2)
        nc.sync.dma_start(out=memory_sb[:, :, chunk_cols(2)], in_=memory_rows[:, :, chunk_cols(2)])
        load_words(wf_words, Wforget_words, 3)
        load_words(ww_words, Wwrite_words, 3)
        nc.sync.dma_start(out=memory_sb[:, :, chunk_cols(3)], in_=memory_rows[:, :, chunk_cols(3)])

        hidden_words = hidden_sb[:].bitcast(F32)
        words_per_pass = K_PASS // 2

        def turn_hidden(t):
            turned = bank()
            for g in range(PASSES):
                for u in range(2):
                    nc.tensor.transpose(
                        turned[:, block_cols(2 * g + u)],
                        hidden_words[:, t, words_per_pass * g + u : words_per_pass * (g + 1) : 2],
                        identity[:],
                    )
            nc.scalar.copy(
                out=grouped[t][:].bitcast(F32),
                in_=turned[:].rearrange("p (g u r) -> p g r u", g=PASSES, u=2),
            )

        def quantise_hidden(t):
            for g in range(PASSES):
                nc.vector.quantize_mx(
                    out=h_codes[:, g, block_cols(t)].bitcast(FP8X4),
                    scales=h_scales[:, g, block_cols(t)],
                    in_=grouped[t][:, g, :, :].rearrange("p r j -> p (r j)"),
                )

        def spread_baddr(c):
            spread = bank()
            for i in range(BLOCKS):
                block = BLOCKS * c + i
                nc.tensor.matmul(
                    out=spread[:, block_cols(i)],
                    lhsT=identity_bf16[:, block : block + 1].to_broadcast([P, P]),
                    rhs=baddr_rows[:],
                    start=True,
                    stop=True,
                )
            nc.scalar.copy(out=baddr_all[:, chunk_cols(c)], in_=spread[:])

        def row_mean_on_vector(t):
            nc.vector.tensor_scalar(
                out=scaled_hidden[:, t, :],
                in0=hidden_sb[:, t, :],
                scalar1=0.5 / HIDDEN,
                scalar2=None,
                op0=ALU.mult,
                op1=ALU.add,
                accum_out=half_mean[:, t : t + 1],
            )

        def row_mean(t):
            nc.scalar.activation(
                out=scaled_hidden[:, t, :],
                in_=hidden_sb[:, t, :],
                func=ACT.Copy,
                scale=0.5 / HIDDEN,
                accum_out=half_mean[:, t : t + 1],
            )


        def addr_passes(t, chunks=range(CHUNKS)):
            banks = []
            for c in chunks:
                acc = bank()
                for g in range(PASSES):
                    nc.tensor.matmul_mx(
                        out=acc[:],
                        lhsT=h_codes[:, g, block_cols(t)].bitcast(FP8X4),
                        lhsT_scale=h_scales[:, g, block_cols(t)],
                        rhs=wa_words[:, g, chunk_cols(c)].bitcast(FP8X4),
                        rhs_scale=planes_a[PLANE_ROWS * g : P, chunk_cols(c)],
                        start=(g == 0),
                        stop=(g == PASSES - 1),
                    )
                banks.append(acc)
            return banks

        def addr_bias(t, banks, chunks=range(CHUNKS)):
            for c, acc in zip(chunks, banks):
                nc.vector.tensor_tensor(
                    out=addr[:, t, chunk_cols(c)], in0=acc[:], in1=baddr_all[:, chunk_cols(c)], op=ALU.add
                )

        def softmax_max(t):
            nc.vector.tensor_reduce(
                out=neg_max[:, t : t + 1], in_=addr[:, t, :], axis=mybir.AxisListType.X, op=ALU.max, negate=True
            )

        def softmax_exp(t):
            nc.scalar.activation(
                out=addr[:, t, :],
                in_=addr[:, t, :],
                func=ACT.Exp,
                bias=neg_max[:, t : t + 1],
                scale=1.0,
                accum_out=exp_sum[:, t : t + 1],
            )

        def softmax_scale(t, engine):
            nc.vector.reciprocal(out=inv_sum[:, t : t + 1], in_=exp_sum[:, t : t + 1])
            engine.tensor_scalar(
                out=addr[:, t, :],
                in0=addr[:, t, :],
                scalar1=inv_sum[:, t : t + 1],
                scalar2=half_mean[:, t : t + 1],
                op0=ALU.mult,
                op1=ALU.mult,
            )

        def halve_on_scalar(c, ts):
            nc.scalar.activation(out=memory_sb[:, ts, chunk_cols(c)], in_=memory_sb[:, ts, chunk_cols(c)], func=ACT.Copy, scale=0.5)

        def halve_memory(c, engine=nc.vector):
            engine.tensor_scalar(
                out=memory_sb[:, :, chunk_cols(c)],
                in0=memory_sb[:, :, chunk_cols(c)],
                scalar1=0.5,
                scalar2=0.0,
                op0=ALU.mult,
                op1=ALU.add,
            )


        gate_tanh = {}
        gate_operands = {"forget": (wf_words, planes_f, 0, 0), "write": (ww_words, planes_w, 0, CHUNKS * BLOCKS)}
        issued = [0]

        def gate_blocks(count):
            for n in range(issued[0], min(issued[0] + count, GATE_BLOCKS)):
                c, gate, i = n // (2 * BLOCKS), ("forget", "write")[n // BLOCKS % 2], n % BLOCKS
                words, planes, first_row, first_bias = gate_operands[gate]
                if i == 0:
                    gate_tanh[(gate, c)] = gate_pool.tile([P, BLOCKS, BATCH], F32, name="gate_t", tag="gate_t")
                block = BLOCKS * c + i
                acc = bank()
                for g in range(PASSES):
                    nc.tensor.matmul_mx(
                        out=acc[:],
                        lhsT=words[:, g, block_cols(block)].bitcast(FP8X4),
                        lhsT_scale=planes[first_row + PLANE_ROWS * g : P, block_cols(block)],
                        rhs=h_codes[:, g, :].bitcast(FP8X4),
                        rhs_scale=h_scales[:, g, :],
                        start=(g == 0),
                        stop=(g == PASSES - 1),
                    )
                nc.scalar.activation(
                    out=gate_tanh[(gate, c)][:, i, :],
                    in_=acc[:],
                    func=ACT.Tanh,
                    bias=half_gate_bias[:, first_bias + block : first_bias + block + 1],
                    scale=0.5,
                )
            issued[0] = min(issued[0] + count, GATE_BLOCKS)

        def turn_back(gate, c, t):
            turned = bank()
            for i in range(BLOCKS):
                nc.tensor.transpose(turned[:, block_cols(i)], gate_tanh[(gate, c)][:, i, block_cols(t)], identity[:])
            return turned

        def one_plus_times(dst, turned, factor):
            nc.vector.scalar_tensor_tensor(out=dst, in0=turned[:], scalar=1.0, in1=factor, op0=ALU.add, op1=ALU.mult)

        def PR(c, row_tiles, blocks, before_last=None):
            turned = {}
            for t, count in zip(row_tiles, blocks):
                for gate in ("forget", "write"):
                    turned[(gate, t)] = turn_back(gate, c, t)
                gate_blocks(count)
            for t in row_tiles:
                if before_last is not None and t == row_tiles[-1]:
                    before_last()
                forget_term = term_pool.tile([P, BANK], F32, name="forget_term", tag="forget_term")
                total = term_pool.tile([P, BANK], F32, name="total", tag="total")
                one_plus_times(forget_term[:], turned[("forget", t)], memory_sb[:, t, chunk_cols(c)])
                one_plus_times(total[:], turned[("write", t)], addr[:, t, chunk_cols(c)])
                last = c == CHUNKS - 1 and t == ROW_TILES - 1
                adder, pieces = (nc.vector, 2) if last else (nc.gpsimd, 1)
                width = BANK // pieces
                for piece in range(pieces):
                    cols = slice(piece * width, (piece + 1) * width)
                    adder.tensor_tensor(out=total[:, cols], in0=total[:, cols], in1=forget_term[:, cols], op=ALU.add)
                    nc.sync.dma_start(
                        out=out_rows[:, t, c * BANK + piece * width : c * BANK + (piece + 1) * width], in_=total[:, cols]
                    )

        def pair(c):
            for t in (0, 1):
                addr_bias(t, addr_passes(t, (c,)), (c,))

        warm = bank()
        for i in range(WARM_UP):
            nc.tensor.matmul(out=warm[:], lhsT=zeros[:, 0:P], rhs=zeros[:], start=True, stop=True)
        turn_hidden(0)
        quantise_hidden(0)
        turn_hidden(1)
        quantise_hidden(1)
        spread_baddr(0)
        spread_baddr(1)
        spread_baddr(2)
        spread_baddr(3)
        pair(0)
        row_mean(0)
        row_mean(1)
        pair(1)
        pair(2)
        turn_hidden(2)
        quantise_hidden(2)
        turn_hidden(3)
        quantise_hidden(3)
        nc.gpsimd.tensor_copy(out=gate_bias_rows_f32[:], in_=gate_bias_rows[:])
        bias_cols = bank()
        nc.tensor.transpose(bias_cols[:, 0:P], gate_bias_rows_f32[:], identity[:])
        nc.vector.tensor_scalar_mul(out=half_gate_bias[:], in0=bias_cols[:, 0:GATE_BLOCKS], scalar1=0.5)
        pair(3)
        row_mean(2)
        gate_blocks(4)
        softmax_max(0)
        banks2 = addr_passes(2)
        softmax_exp(0)
        gate_blocks(3)
        halve_memory(0, nc.gpsimd)
        halve_memory(1, nc.gpsimd)
        softmax_max(1)
        softmax_exp(1)
        addr_bias(2, banks2)
        banks3 = addr_passes(3)
        softmax_scale(0, nc.gpsimd)
        softmax_max(2)
        softmax_scale(1, nc.gpsimd)
        gate_blocks(1)
        softmax_exp(2)
        gate_blocks(3)
        addr_bias(3, banks3)
        gate_blocks(4)
        softmax_scale(2, nc.gpsimd)
        softmax_max(3)
        PR(0, (0, 1), (1, 2))
        softmax_exp(3)
        PR(1, (0, 1), (0, 3))
        row_mean_on_vector(3)
        PR(0, (2, 3), (0, 3), lambda: softmax_scale(ROW_TILES - 1, nc.vector))
        halve_on_scalar(2, slice(0, 2))
        PR(1, (2, 3), (0, 3))
        halve_on_scalar(2, slice(2, 4))
        PR(2, (0, 1), (0, 3))
        halve_on_scalar(3, slice(0, 2))
        PR(2, (2, 3), (0, 2))
        halve_on_scalar(3, slice(2, 4))
        PR(3, (0, 1), (0, 0))
        PR(3, (2, 3), (0, 0))
